import numpy as np
import ml_dtypes


def mxq(x, axis, fmt="e4m3"):
    dtype, down = {"e4m3": (ml_dtypes.float8_e4m3fn, 7), "e5m2": (ml_dtypes.float8_e5m2, 14)}[fmt]
    v = np.moveaxis(np.asarray(x, np.float32).astype(ml_dtypes.bfloat16).astype(np.float64), axis, -1)
    blocks = v.reshape(v.shape[:-1] + (-1, 32))
    amax = np.abs(blocks).max(-1, keepdims=True)
    byte = np.maximum(np.where(amax > 0, np.frexp(amax)[1] - 1 + 127, 0) - down, 1)
    scale = np.exp2(byte - 127.0)
    codes = (blocks / scale).astype(np.float32).astype(dtype).astype(np.float64)
    return np.moveaxis((codes * scale).reshape(v.shape), -1, axis)


WIDE = False


def mx_kscale(k):
    if not WIDE:
        return np.ones(k)
    levels = np.array([10, -10, 5, -5, 0])
    a = np.random.permutation(np.resize(levels, k // 512 * 4)).reshape(k // 512, 4)
    idx = np.arange(k)
    return np.exp2(a[idx // 512, idx % 128 // 32])


BF16 = ml_dtypes.bfloat16


def bf(x):
    return np.asarray(x, np.float32).astype(BF16)


def f64(x):
    return np.asarray(x).astype(np.float64)


E2M1 = np.array([0.0, 0.5, 1.0, 1.5, 2.0, 3.0, 4.0, 6.0, -0.0, -0.5, -1.0, -1.5, -2.0, -3.0, -4.0, -6.0])


def pack_weight(w, fmt):
    k, n = w.shape
    w = f64(bf(w)).reshape(k // 32, 32, n)
    amax = np.abs(w).max(1)
    if fmt == "e4m3":
        byte = np.frexp(amax)[1] - 1 + 127 - 7
    else:
        mant, ex = np.frexp(amax / 6.0)
        byte = np.where(mant > 0.5, ex, ex - 1) + 127
    byte = np.clip(np.where(amax > 0, byte, 1), 1, 254)
    scaled = (w * np.exp2(127.0 - byte)[:, None, :]).reshape(k, n).astype(np.float32)
    by_word = np.ascontiguousarray(scaled.reshape(k // 512, 128, 4, n).transpose(0, 1, 3, 2))
    if fmt == "e4m3":
        words = by_word.astype(ml_dtypes.float8_e4m3fn).view(np.uint8)
    else:
        c = by_word.astype(ml_dtypes.float4_e2m1fn).view(np.uint8) & 0xF
        words = c[..., 0::2] | (c[..., 1::2] << 4)
    return np.ascontiguousarray(words), np.ascontiguousarray(byte.astype(np.uint8).reshape(k // 512, 16, n))


def unpack_weight(words, scales, fmt):
    g, p, n, _ = words.shape
    if fmt == "e4m3":
        vals = np.ascontiguousarray(words).view(ml_dtypes.float8_e4m3fn).astype(np.float64)
    else:
        nib = np.empty((g, p, n, 4), np.uint8)
        nib[..., 0::2] = words & 0xF
        nib[..., 1::2] = words >> 4
        vals = E2M1[nib]
    vals = vals * np.repeat(np.exp2(scales.astype(np.float64) - 127.0), 8, axis=1)[..., None]
    return vals.transpose(0, 1, 3, 2).reshape(g * 512, n)


B, ND, NS, D = 2, 128, 128, 3072
NUM_ITERS = 5
REG = 0.1
EPS = 1e-12
FMT = "e4m3"


def l2_normalize(v):
    n = np.sqrt(np.sum(v * v, axis=-1, keepdims=True))
    return v / np.maximum(n, EPS)


def logsumexp(v, axis):
    m = np.max(v, axis=axis, keepdims=True)
    return m + np.log(np.sum(np.exp(v - m), axis=axis, keepdims=True))


def setup_inputs():
    s, t = mx_kscale(D), mx_kscale(D)
    c0 = np.random.standard_normal((B, 1, D))
    c1 = np.random.standard_normal((B, 1, D))
    gd = np.random.random((B, ND, 1)) < 0.7
    gs = np.random.random((B, NS, 1)) < 0.3
    drone = np.random.standard_normal((B, ND, D)) + 1.44 * np.where(gd, c0, c1)
    sat = np.random.standard_normal((B, NS, D)) + 1.44 * np.where(gs, c0, c1)
    w0 = np.random.standard_normal((D, D))
    wq = (w0 + 0.5 * np.random.standard_normal((D, D))) * 0.9 / np.sqrt(D)
    wk = (w0 + 0.5 * np.random.standard_normal((D, D))) * 0.9 / np.sqrt(D)
    wq_words, wq_scales = pack_weight((wq / s).T, FMT)
    wk_words, wk_scales = pack_weight((wk / t).T, FMT)
    return {"drone_tokens": bf(drone * s), "sat_tokens": bf(sat * t),
            "Wq_words": wq_words, "Wq_scales": wq_scales, "bq": bf(np.random.standard_normal(D) * 0.5),
            "Wk_words": wk_words, "Wk_scales": wk_scales, "bk": bf(np.random.standard_normal(D) * 0.5)}


def reference(drone_tokens, sat_tokens, Wq_words, Wq_scales, bq, Wk_words, Wk_scales, bk):
    q = l2_normalize((mxq(f64(drone_tokens), 2, "e4m3") @ unpack_weight(Wq_words, Wq_scales, FMT)) + f64(bq))
    k = l2_normalize((mxq(f64(sat_tokens), 2, "e4m3") @ unpack_weight(Wk_words, Wk_scales, FMT)) + f64(bk))
    cost = 1.0 - (mxq(q, 2, "e4m3") @ mxq(k, 2, "e4m3").transpose(0, 2, 1))
    M = -cost / REG
    for _ in range(NUM_ITERS):
        M = M - logsumexp(M, 2)
        M = M - logsumexp(M, 1)
    transport_plan = np.exp(M)
    ot_cost = np.mean(np.sum(transport_plan * cost, axis=(1, 2)))
    return transport_plan, ot_cost

@@ -1,0 +1,253 @@
+from contextlib import ExitStack
+
+import concourse.mybir as mybir
+from concourse.masks import make_identity
+
+F32 = mybir.dt.float32
+BF16 = mybir.dt.bfloat16
+I32 = mybir.dt.int32
+U32 = mybir.dt.uint32
+U8 = mybir.dt.uint8
+FP8X4 = mybir.dt.float8_e4m3fn_x4
+ALU = mybir.AluOpType
+ACT = mybir.ActivationFunctionType
+AXIS = mybir.AxisListType
+
+P = 128
+BATCH = 2
+D = 3072
+K_PASS = 512
+GROUPS = D // K_PASS
+BANK = 512
+RANGE = 2 * BANK
+PLANES_PER_SLOT = 4
+NUM_ITERS = 5
+INV_REG = 10.0
+EPS = 1e-12
+
+FLOPS = 2 * (2 * BATCH * P * D * D) + 2 * BATCH * P * P * D
+
+
+def load_scale_planes(nc, planes, scales):
+    words = scales.bitcast(I32)
+    for first in range(0, GROUPS, PLANES_PER_SLOT):
+        count = min(PLANES_PER_SLOT, GROUPS - first)
+        for quadrant in range(4):
+            nc.sync.dma_start(
+                out=planes[32 * quadrant : 32 * quadrant + 4 * count, first // PLANES_PER_SLOT, :].bitcast(I32),
+                in_=words[first : first + count, 4 * quadrant : 4 * quadrant + 4, :],
+            )
+
+
+def scale_plane(planes, g, cols):
+    return planes[4 * (g % PLANES_PER_SLOT) : P, g // PLANES_PER_SLOT, cols]
+
+
+def pack_group(nc, psum, stage, identity, rows, g, codes, scales):
+    flipped = psum.tile([P, BATCH, 2, P], F32, tag="bank")
+    for b in range(BATCH):
+        words = rows[b][:].bitcast(F32)
+        for u in range(2):
+            nc.tensor.transpose(
+                flipped[:, b, u, :], words[:, (K_PASS // 2) * g + u : (K_PASS // 2) * (g + 1) : 2], identity[:]
+            )
+    grouped = stage.tile([P, BATCH, P, 2], F32, align_bytes=64)
+    nc.scalar.copy(out=grouped[:], in_=flipped[:].rearrange("p b u r -> p b r u"))
+    nc.vector.quantize_mx(
+        out=codes[:, g, :].bitcast(FP8X4),
+        scales=scales[:, g, :],
+        in_=grouped[:].rearrange("p b r u -> p (b r u)").bitcast(BF16),
+    )
+
+
+def project(nc, psum, wpool, stage, w_words, planes, x_codes, x_scales, bias, y, sumsq):
+    words = w_words.rearrange("g p n t -> g p (n t)").bitcast(I32)
+    for first in range(0, D, RANGE):
+        acc = [[psum.tile([P, BANK], F32, tag="bank", name="acc%d%d" % (b, h)) for h in range(2)] for b in range(BATCH)]
+        for g in range(GROUPS):
+            chunk = wpool.tile([P, RANGE], U32, align_bytes=64)
+            nc.sync.dma_start(out=chunk[:].bitcast(I32), in_=words[g, :, first : first + RANGE])
+            for b in range(BATCH):
+                for h in range(2):
+                    nc.tensor.matmul_mx(
+                        out=acc[b][h][:],
+                        lhsT=x_codes[:, g, P * b : P * (b + 1)].bitcast(FP8X4),
+                        lhsT_scale=x_scales[:, g, P * b : P * (b + 1)],
+                        rhs=chunk[:, BANK * h : BANK * (h + 1)].bitcast(FP8X4),
+                        rhs_scale=scale_plane(planes, g, slice(first + BANK * h, first + BANK * (h + 1))),
+                        start=(g == 0),
+                        stop=(g == GROUPS - 1),
+                    )
+        for b in range(BATCH):
+            for h in range(2):
+                cols = slice(first + BANK * h, first + BANK * (h + 1))
+                nc.vector.tensor_tensor(out=y[b][:, cols], in0=acc[b][h][:], in1=bias[:, cols], op=ALU.add)
+                squares = stage.tile([P, BANK], BF16)
+                block = (first + BANK * h) // BANK
+                nc.scalar.activation(
+                    out=squares[:], in_=y[b][:, cols], func=ACT.Square, accum_out=sumsq[:, b, block : block + 1]
+                )
+
+
+def inverse_norms(nc, small, sumsq, minus_half, name):
+    total = small.tile([P, BATCH], F32, name=name + "_total")
+    nc.vector.tensor_reduce(out=total[:], in_=sumsq[:], axis=AXIS.X, op=ALU.add)
+    nc.vector.tensor_scalar_max(out=total[:], in0=total[:], scalar1=EPS * EPS)
+    inv = small.tile([P, BATCH], F32, name=name + "_inv")
+    nc.gpsimd.tensor_tensor(out=inv[:], in0=total[:], in1=minus_half[:], op=ALU.pow)
+    return inv
+
+
+def normalise_group(nc, y, inv, rows, g):
+    cols = slice(K_PASS * g, K_PASS * (g + 1))
+    for b in range(BATCH):
+        nc.vector.tensor_scalar_mul(out=rows[b][:, cols], in0=y[b][:, cols], scalar1=inv[:, b : b + 1])
+
+
+def tile_sinkhornot_w_kernel(
+    tc, drone_tokens, sat_tokens, Wq_words, Wq_scales, bq, Wk_words, Wk_scales, bk, out_0, out_1
+):
+    nc = tc.nc
+    with ExitStack() as ctx:
+        const = ctx.enter_context(tc.tile_pool(name="const", bufs=1))
+        keep = ctx.enter_context(tc.tile_pool(name="keep", bufs=1))
+        small = ctx.enter_context(tc.tile_pool(name="small", bufs=1))
+        rowpool = ctx.enter_context(tc.tile_pool(name="rowpool", bufs=4))
+        ypool = ctx.enter_context(tc.tile_pool(name="ypool", bufs=4))
+        wpool = ctx.enter_context(tc.tile_pool(name="wpool", bufs=14))
+        stage = ctx.enter_context(tc.tile_pool(name="stage", bufs=3))
+        psum = ctx.enter_context(tc.psum_pool(name="psum", bufs=8))
+
+        planes_q = keep.tile([P, 2, D], U8, align_bytes=64)
+        planes_k = keep.tile([P, 2, D], U8, align_bytes=64)
+        nc.vector.memset(planes_q[:].bitcast(I32), 0)
+        nc.vector.memset(planes_k[:].bitcast(I32), 0)
+        bias_row = keep.tile([P, 2 * D], BF16)
+        nc.vector.memset(bias_row[:], 0.0)
+        identity = const.tile([P, P], F32)
+        make_identity(nc, identity[:])
+        ones = const.tile([P, P], BF16)
+        nc.gpsimd.memset(ones[:], 1.0)
+        minus_half = const.tile([P, BATCH], F32)
+        nc.gpsimd.memset(minus_half[:], -0.5)
+        warm = const.tile([P, 1], F32)
+        nc.gpsimd.memset(warm[:], 0.0)
+        nc.scalar.activation(out=warm[:], in_=warm[:], func=ACT.Exp)
+
+        drone = [rowpool.tile([P, D], BF16, tag="rows", name="drone%d" % b) for b in range(BATCH)]
+        sat = [rowpool.tile([P, D], BF16, tag="rows", name="sat%d" % b) for b in range(BATCH)]
+        for b in range(BATCH):
+            nc.sync.dma_start(out=drone[b][:], in_=drone_tokens[b])
+        for b in range(BATCH):
+            nc.sync.dma_start(out=sat[b][:], in_=sat_tokens[b])
+        nc.sync.dma_start(out=bias_row[0:1, 0:D], in_=bq.unsqueeze(0))
+        nc.sync.dma_start(out=bias_row[0:1, D : 2 * D], in_=bk.unsqueeze(0))
+        load_scale_planes(nc, planes_q, Wq_scales)
+        load_scale_planes(nc, planes_k, Wk_scales)
+
+        packed = {}
+        for name in ("drone", "sat", "q", "k"):
+            packed[name] = (
+                keep.tile([P, GROUPS, BATCH * P], U32, align_bytes=64, name=name + "_codes"),
+                keep.tile([P, GROUPS, BATCH * P], U8, align_bytes=64, name=name + "_scales"),
+            )
+        for name, rows in (("drone", drone), ("sat", sat)):
+            for g in range(GROUPS):
+                pack_group(nc, psum, stage, identity, rows, g, packed[name][0], packed[name][1])
+
+        bias = keep.tile([P, 2 * D], BF16)
+        for first in range(0, 2 * D, BANK):
+            spread = psum.tile([P, BANK], F32, tag="bank")
+            nc.tensor.matmul(spread[:], lhsT=ones[:], rhs=bias_row[:, first : first + BANK], start=True, stop=True)
+            nc.scalar.copy(out=bias[:, first : first + BANK], in_=spread[:])
+
+        y_q = [ypool.tile([P, D], F32, tag="y", name="y_q%d" % b) for b in range(BATCH)]
+        sumsq_q = small.tile([P, BATCH, D // BANK], F32)
+        project(nc, psum, wpool, stage, Wq_words, planes_q, packed["drone"][0], packed["drone"][1], bias[:, 0:D], y_q, sumsq_q)
+        inv_q = inverse_norms(nc, small, sumsq_q, minus_half, "q")
+        q_rows = [rowpool.tile([P, D], BF16, tag="rows", name="q_rows%d" % b) for b in range(BATCH)]
+        for g in range(GROUPS):
+            normalise_group(nc, y_q, inv_q, q_rows, g)
+            pack_group(nc, psum, stage, identity, q_rows, g, packed["q"][0], packed["q"][1])
+
+        y_k = [ypool.tile([P, D], F32, tag="y", name="y_k%d" % b) for b in range(BATCH)]
+        sumsq_k = small.tile([P, BATCH, D // BANK], F32)
+        project(nc, psum, wpool, stage, Wk_words, planes_k, packed["sat"][0], packed["sat"][1], bias[:, D : 2 * D], y_k, sumsq_k)
+        inv_k = inverse_norms(nc, small, sumsq_k, minus_half, "k")
+        k_rows = [rowpool.tile([P, D], BF16, tag="rows", name="k_rows%d" % b) for b in range(BATCH)]
+        sim = [psum.tile([P, P], F32, tag="bank", name="sim%d" % b) for b in range(BATCH)]
+        sim_t = [psum.tile([P, P], F32, tag="bank", name="sim_t%d" % b) for b in range(BATCH)]
+        for g in range(GROUPS):
+            normalise_group(nc, y_k, inv_k, k_rows, g)
+            pack_group(nc, psum, stage, identity, k_rows, g, packed["k"][0], packed["k"][1])
+            for b in range(BATCH):
+                tokens = slice(P * b, P * (b + 1))
+                for out, left, right in ((sim[b], "q", "k"), (sim_t[b], "k", "q")):
+                    nc.tensor.matmul_mx(
+                        out=out[:],
+                        lhsT=packed[left][0][:, g, tokens].bitcast(FP8X4),
+                        lhsT_scale=packed[left][1][:, g, tokens],
+                        rhs=packed[right][0][:, g, tokens].bitcast(FP8X4),
+                        rhs_scale=packed[right][1][:, g, tokens],
+                        start=(g == 0),
+                        stop=(g == GROUPS - 1),
+                    )
+
+        kern = small.tile([P, BATCH, P], F32)
+        kern_t = small.tile([P, BATCH, P], F32)
+        cost = small.tile([P, BATCH, P], F32)
+        kern_cost = small.tile([P, BATCH, P], F32)
+        row_sum = small.tile([P, BATCH], F32)
+        for b in range(BATCH):
+            nc.scalar.activation(
+                out=kern[:, b, :], in_=sim[b][:], func=ACT.Exp, scale=INV_REG, bias=-INV_REG,
+                accum_out=row_sum[:, b : b + 1],
+            )
+        for b in range(BATCH):
+            nc.scalar.activation(out=kern_t[:, b, :], in_=sim_t[b][:], func=ACT.Exp, scale=INV_REG, bias=-INV_REG)
+        for b in range(BATCH):
+            nc.scalar.activation(out=cost[:, b, :], in_=sim[b][:], func=ACT.Copy, scale=-1.0, bias=1.0)
+        nc.gpsimd.tensor_tensor(out=kern_cost[:], in0=kern[:], in1=cost[:], op=ALU.mult)
+
+        u = small.tile([P, BATCH], F32, name="u0")
+        nc.vector.reciprocal(out=u[:], in_=row_sum[:])
+        for it in range(1, NUM_ITERS):
+            col_sum = psum.tile([P, BATCH], F32, tag="bank")
+            for b in range(BATCH):
+                nc.tensor.matmul(col_sum[:, b : b + 1], lhsT=kern[:, b, :], rhs=u[:, b : b + 1], start=True, stop=True)
+            v = small.tile([P, BATCH], F32, name="v%d" % it)
+            nc.vector.reciprocal(out=v[:], in_=col_sum[:])
+            row_sum_ps = psum.tile([P, BATCH], F32, tag="bank")
+            for b in range(BATCH):
+                nc.tensor.matmul(row_sum_ps[:, b : b + 1], lhsT=kern_t[:, b, :], rhs=v[:, b : b + 1], start=True, stop=True)
+            u = small.tile([P, BATCH], F32, name="u%d" % it)
+            nc.vector.reciprocal(out=u[:], in_=row_sum_ps[:])
+
+        col_sum_all = psum.tile([P, BATCH, P], F32, tag="bank")
+        cost_sum_all = psum.tile([P, BATCH, P], F32, tag="bank")
+        for b in range(BATCH):
+            u_all = u[:, b : b + 1].to_broadcast([P, P])
+            nc.tensor.matmul(col_sum_all[:, b, :], lhsT=u_all, rhs=kern[:, b, :], start=True, stop=True)
+        for b in range(BATCH):
+            u_all = u[:, b : b + 1].to_broadcast([P, P])
+            nc.tensor.matmul(cost_sum_all[:, b, :], lhsT=u_all, rhs=kern_cost[:, b, :], start=True, stop=True)
+        v_all = small.tile([P, BATCH, P], F32)
+        nc.vector.reciprocal(out=v_all[:], in_=col_sum_all[:])
+        plan = small.tile([P, BATCH, P], F32)
+        for b in range(BATCH):
+            nc.vector.scalar_tensor_tensor(
+                out=plan[:, b, :], in0=kern[:, b, :], scalar=u[:, b : b + 1], in1=v_all[:, b, :],
+                op0=ALU.mult, op1=ALU.mult,
+            )
+        nc.sync.dma_start(out=out_0.rearrange("b i j -> i b j"), in_=plan[:])
+
+        terms = small.tile([P, BATCH, P], F32)
+        ot_cost = small.tile([P, 1], F32)
+        nc.vector.scalar_tensor_tensor(
+            out=terms[:], in0=cost_sum_all[:], scalar=1.0 / BATCH, in1=v_all[:], op0=ALU.mult, op1=ALU.mult,
+            accum_out=ot_cost[:],
+        )
+        ot_dst = out_1
+        for missing in range(2 - out_1.ndim):
+            ot_dst = ot_dst.unsqueeze(0)
+        nc.sync.dma_start(out=ot_dst, in_=ot_cost[0:1, 0:1])

@@ -18,9 +18,11 @@ BATCH = 2
 D = 3072
 K_PASS = 512
 GROUPS = D // K_PASS
+WORDS = K_PASS // 2
 BANK = 512
 RANGE = 2 * BANK
 PLANES_PER_SLOT = 4
+QUANT_LAG = 2
 NUM_ITERS = 5
 INV_REG = 10.0
 EPS = 1e-12
@@ -43,16 +45,27 @@ def scale_plane(planes, g, cols):
     return planes[4 * (g % PLANES_PER_SLOT) : P, g // PLANES_PER_SLOT, cols]
 
 
-def pack_group(nc, psum, stage, identity, rows, g, codes, scales):
+def every_second_word(g, u):
+    return slice(WORDS * g + u, WORDS * (g + 1), 2)
+
+
+def half_of_the_words(g, u):
+    return slice(WORDS * g + P * u, WORDS * g + P * (u + 1))
+
+
+def flip_group(nc, psum, stage, identity, rows, word_cols, g, copy):
     flipped = psum.tile([P, BATCH, 2, P], F32, tag="bank")
     for b in range(BATCH):
         words = rows[b][:].bitcast(F32)
         for u in range(2):
-            nc.tensor.transpose(
-                flipped[:, b, u, :], words[:, (K_PASS // 2) * g + u : (K_PASS // 2) * (g + 1) : 2], identity[:]
-            )
+            nc.tensor.transpose(flipped[:, b, u, :], words[:, word_cols(g, u)], identity[:])
     grouped = stage.tile([P, BATCH, P, 2], F32, align_bytes=64)
-    nc.scalar.copy(out=grouped[:], in_=flipped[:].rearrange("p b u r -> p b r u"))
+    copy(out=grouped[:], in_=flipped[:].rearrange("p b u r -> p b r u"))
+    return grouped
+
+
+def quantise_group(nc, grouped, g, packed):
+    codes, scales = packed
     nc.vector.quantize_mx(
         out=codes[:, g, :].bitcast(FP8X4),
         scales=scales[:, g, :],
@@ -60,33 +73,39 @@ def pack_group(nc, psum, stage, identity, rows, g, codes, scales):
     )
 
 
-def project(nc, psum, wpool, stage, w_words, planes, x_codes, x_scales, bias, y, sumsq):
+def open_range(psum):
+    return [[psum.tile([P, BANK], F32, tag="bank", name="acc%d%d" % (b, h)) for h in range(2)] for b in range(BATCH)]
+
+
+def multiply_range(nc, wpool, acc, w_words, planes, x_packed, first):
     words = w_words.rearrange("g p n t -> g p (n t)").bitcast(I32)
-    for first in range(0, D, RANGE):
-        acc = [[psum.tile([P, BANK], F32, tag="bank", name="acc%d%d" % (b, h)) for h in range(2)] for b in range(BATCH)]
-        for g in range(GROUPS):
-            chunk = wpool.tile([P, RANGE], U32, align_bytes=64)
-            nc.sync.dma_start(out=chunk[:].bitcast(I32), in_=words[g, :, first : first + RANGE])
-            for b in range(BATCH):
-                for h in range(2):
-                    nc.tensor.matmul_mx(
-                        out=acc[b][h][:],
-                        lhsT=x_codes[:, g, P * b : P * (b + 1)].bitcast(FP8X4),
-                        lhsT_scale=x_scales[:, g, P * b : P * (b + 1)],
-                        rhs=chunk[:, BANK * h : BANK * (h + 1)].bitcast(FP8X4),
-                        rhs_scale=scale_plane(planes, g, slice(first + BANK * h, first + BANK * (h + 1))),
-                        start=(g == 0),
-                        stop=(g == GROUPS - 1),
-                    )
+    x_codes, x_scales = x_packed
+    for g in range(GROUPS):
+        chunk = wpool.tile([P, RANGE], U32, align_bytes=64)
+        nc.sync.dma_start(out=chunk[:].bitcast(I32), in_=words[g, :, first : first + RANGE])
         for b in range(BATCH):
             for h in range(2):
-                cols = slice(first + BANK * h, first + BANK * (h + 1))
-                nc.vector.tensor_tensor(out=y[b][:, cols], in0=acc[b][h][:], in1=bias[:, cols], op=ALU.add)
-                squares = stage.tile([P, BANK], BF16)
-                block = (first + BANK * h) // BANK
-                nc.scalar.activation(
-                    out=squares[:], in_=y[b][:, cols], func=ACT.Square, accum_out=sumsq[:, b, block : block + 1]
+                nc.tensor.matmul_mx(
+                    out=acc[b][h][:],
+                    lhsT=x_codes[:, g, P * b : P * (b + 1)].bitcast(FP8X4),
+                    lhsT_scale=x_scales[:, g, P * b : P * (b + 1)],
+                    rhs=chunk[:, BANK * h : BANK * (h + 1)].bitcast(FP8X4),
+                    rhs_scale=scale_plane(planes, g, slice(first + BANK * h, first + BANK * (h + 1))),
+                    start=(g == 0),
+                    stop=(g == GROUPS - 1),
                 )
+
+
+def empty_range(nc, stage, acc, bias, y, sumsq, first):
+    for b in range(BATCH):
+        for h in range(2):
+            cols = slice(first + BANK * h, first + BANK * (h + 1))
+            nc.vector.tensor_tensor(out=y[b][:, cols], in0=acc[b][h][:], in1=bias[:, cols], op=ALU.add)
+            squares = stage.tile([P, BANK], BF16)
+            block = (first + BANK * h) // BANK
+            nc.scalar.activation(
+                out=squares[:], in_=y[b][:, cols], func=ACT.Square, accum_out=sumsq[:, b, block : block + 1]
+            )
 
 
 def inverse_norms(nc, small, sumsq, minus_half, name):
@@ -98,10 +117,13 @@ def inverse_norms(nc, small, sumsq, minus_half, name):
     return inv
 
 
-def normalise_group(nc, y, inv, rows, g):
+def normalise_group(nc, y, inv, rows, g, on_scalar=False):
     cols = slice(K_PASS * g, K_PASS * (g + 1))
     for b in range(BATCH):
-        nc.vector.tensor_scalar_mul(out=rows[b][:, cols], in0=y[b][:, cols], scalar1=inv[:, b : b + 1])
+        if on_scalar:
+            nc.scalar.activation(out=rows[b][:, cols], in_=y[b][:, cols], func=ACT.Copy, scale=inv[:, b : b + 1])
+        else:
+            nc.vector.tensor_scalar_mul(out=rows[b][:, cols], in0=y[b][:, cols], scalar1=inv[:, b : b + 1])
 
 
 def tile_sinkhornot_w_kernel(
@@ -112,18 +134,20 @@ def tile_sinkhornot_w_kernel(
         const = ctx.enter_context(tc.tile_pool(name="const", bufs=1))
         keep = ctx.enter_context(tc.tile_pool(name="keep", bufs=1))
         small = ctx.enter_context(tc.tile_pool(name="small", bufs=1))
+        turn = ctx.enter_context(tc.tile_pool(name="turn", bufs=2))
         rowpool = ctx.enter_context(tc.tile_pool(name="rowpool", bufs=4))
         ypool = ctx.enter_context(tc.tile_pool(name="ypool", bufs=4))
-        wpool = ctx.enter_context(tc.tile_pool(name="wpool", bufs=14))
-        stage = ctx.enter_context(tc.tile_pool(name="stage", bufs=3))
+        wpool = ctx.enter_context(tc.tile_pool(name="wpool", bufs=12))
+        stage = ctx.enter_context(tc.tile_pool(name="stage", bufs=GROUPS))
         psum = ctx.enter_context(tc.psum_pool(name="psum", bufs=8))
+        ctx.enter_context(tc.manual_schedule())
 
         planes_q = keep.tile([P, 2, D], U8, align_bytes=64)
         planes_k = keep.tile([P, 2, D], U8, align_bytes=64)
+        bias_row = keep.tile([P, 2 * D], BF16)
+        nc.vector.memset(bias_row[:].bitcast(I32), 0)
         nc.vector.memset(planes_q[:].bitcast(I32), 0)
         nc.vector.memset(planes_k[:].bitcast(I32), 0)
-        bias_row = keep.tile([P, 2 * D], BF16)
-        nc.vector.memset(bias_row[:], 0.0)
         identity = const.tile([P, P], F32)
         make_identity(nc, identity[:])
         ones = const.tile([P, P], BF16)
@@ -151,35 +175,65 @@ def tile_sinkhornot_w_kernel(
                 keep.tile([P, GROUPS, BATCH * P], U32, align_bytes=64, name=name + "_codes"),
                 keep.tile([P, GROUPS, BATCH * P], U8, align_bytes=64, name=name + "_scales"),
             )
+        copies = (nc.scalar.copy, nc.vector.tensor_copy)
         for name, rows in (("drone", drone), ("sat", sat)):
-            for g in range(GROUPS):
-                pack_group(nc, psum, stage, identity, rows, g, packed[name][0], packed[name][1])
+            grouped = {}
+            for g in range(GROUPS + QUANT_LAG):
+                if g < GROUPS:
+                    grouped[g] = flip_group(nc, psum, stage, identity, rows, every_second_word, g, copies[g % 2])
+                if g >= QUANT_LAG:
+                    quantise_group(nc, grouped[g - QUANT_LAG], g - QUANT_LAG, packed[name])
 
         bias = keep.tile([P, 2 * D], BF16)
-        for first in range(0, 2 * D, BANK):
-            spread = psum.tile([P, BANK], F32, tag="bank")
-            nc.tensor.matmul(spread[:], lhsT=ones[:], rhs=bias_row[:, first : first + BANK], start=True, stop=True)
-            nc.scalar.copy(out=bias[:, first : first + BANK], in_=spread[:])
+        for first in range(0, 2 * D, 2 * BANK):
+            spread = psum.tile([P, 2 * BANK], BF16, tag="bank")
+            for h in range(2):
+                nc.tensor.matmul(
+                    spread[:, BANK * h : BANK * (h + 1)], lhsT=ones[:],
+                    rhs=bias_row[:, first + BANK * h : first + BANK * (h + 1)], start=True, stop=True,
+                )
+            nc.scalar.copy(out=bias[:, first : first + 2 * BANK], in_=spread[:])
 
         y_q = [ypool.tile([P, D], F32, tag="y", name="y_q%d" % b) for b in range(BATCH)]
         sumsq_q = small.tile([P, BATCH, D // BANK], F32)
-        project(nc, psum, wpool, stage, Wq_words, planes_q, packed["drone"][0], packed["drone"][1], bias[:, 0:D], y_q, sumsq_q)
+        for first in range(0, D, RANGE):
+            acc = open_range(psum)
+            multiply_range(nc, wpool, acc, Wq_words, planes_q, packed["drone"], first)
+            empty_range(nc, stage, acc, bias[:, 0:D], y_q, sumsq_q, first)
         inv_q = inverse_norms(nc, small, sumsq_q, minus_half, "q")
         q_rows = [rowpool.tile([P, D], BF16, tag="rows", name="q_rows%d" % b) for b in range(BATCH)]
         for g in range(GROUPS):
             normalise_group(nc, y_q, inv_q, q_rows, g)
-            pack_group(nc, psum, stage, identity, q_rows, g, packed["q"][0], packed["q"][1])
 
         y_k = [ypool.tile([P, D], F32, tag="y", name="y_k%d" % b) for b in range(BATCH)]
         sumsq_k = small.tile([P, BATCH, D // BANK], F32)
-        project(nc, psum, wpool, stage, Wk_words, planes_k, packed["sat"][0], packed["sat"][1], bias[:, D : 2 * D], y_k, sumsq_k)
+        for first in range(0, D, RANGE):
+            acc = open_range(psum)
+            multiply_range(nc, wpool, acc, Wk_words, planes_k, packed["sat"], first)
+            if first == RANGE:
+                grouped = [
+                    flip_group(nc, psum, stage, identity, q_rows, half_of_the_words, g, nc.scalar.copy)
+                    for g in range(GROUPS)
+                ]
+            empty_range(nc, stage, acc, bias[:, D : 2 * D], y_k, sumsq_k, first)
+            if first == RANGE:
+                for g in range(GROUPS):
+                    quantise_group(nc, grouped[g], g, packed["q"])
         inv_k = inverse_norms(nc, small, sumsq_k, minus_half, "k")
         k_rows = [rowpool.tile([P, D], BF16, tag="rows", name="k_rows%d" % b) for b in range(BATCH)]
+        normalise_group(nc, y_k, inv_k, k_rows, GROUPS - 1, on_scalar=True)
+        grouped = {}
+        for g in range(GROUPS + QUANT_LAG):
+            if g < GROUPS - 1:
+                normalise_group(nc, y_k, inv_k, k_rows, g)
+            if g < GROUPS:
+                grouped[g] = flip_group(nc, psum, stage, identity, k_rows, half_of_the_words, g, nc.scalar.copy)
+            if g >= QUANT_LAG:
+                quantise_group(nc, grouped[g - QUANT_LAG], g - QUANT_LAG, packed["k"])
+
         sim = [psum.tile([P, P], F32, tag="bank", name="sim%d" % b) for b in range(BATCH)]
         sim_t = [psum.tile([P, P], F32, tag="bank", name="sim_t%d" % b) for b in range(BATCH)]
         for g in range(GROUPS):
-            normalise_group(nc, y_k, inv_k, k_rows, g)
-            pack_group(nc, psum, stage, identity, k_rows, g, packed["k"][0], packed["k"][1])
             for b in range(BATCH):
                 tokens = slice(P * b, P * (b + 1))
                 for out, left, right in ((sim[b], "q", "k"), (sim_t[b], "k", "q")):
@@ -193,60 +247,59 @@ def tile_sinkhornot_w_kernel(
                         stop=(g == GROUPS - 1),
                     )
 
-        kern = small.tile([P, BATCH, P], F32)
-        kern_t = small.tile([P, BATCH, P], F32)
-        cost = small.tile([P, BATCH, P], F32)
-        kern_cost = small.tile([P, BATCH, P], F32)
-        row_sum = small.tile([P, BATCH], F32)
+        kern = [small.tile([P, P], F32, name="kern%d" % b) for b in range(BATCH)]
+        kern_t = [small.tile([P, P], F32, name="kern_t%d" % b) for b in range(BATCH)]
+        cost = [small.tile([P, P], F32, name="cost%d" % b) for b in range(BATCH)]
+        kern_cost = [small.tile([P, P], F32, name="kern_cost%d" % b) for b in range(BATCH)]
+        u = [None, None]
+        v = [None, None]
         for b in range(BATCH):
+            row_sum = turn.tile([P, 1], F32, name="first_row_sum%d" % b)
             nc.scalar.activation(
-                out=kern[:, b, :], in_=sim[b][:], func=ACT.Exp, scale=INV_REG, bias=-INV_REG,
-                accum_out=row_sum[:, b : b + 1],
+                out=kern[b][:], in_=sim[b][:], func=ACT.Exp, scale=INV_REG, bias=-INV_REG, accum_out=row_sum[:]
             )
+            u[b] = turn.tile([P, 1], F32, name="u%d" % b)
+            nc.vector.reciprocal(out=u[b][:], in_=row_sum[:])
         for b in range(BATCH):
-            nc.scalar.activation(out=kern_t[:, b, :], in_=sim_t[b][:], func=ACT.Exp, scale=INV_REG, bias=-INV_REG)
+            nc.scalar.activation(out=kern_t[b][:], in_=sim_t[b][:], func=ACT.Exp, scale=INV_REG, bias=-INV_REG)
         for b in range(BATCH):
-            nc.scalar.activation(out=cost[:, b, :], in_=sim[b][:], func=ACT.Copy, scale=-1.0, bias=1.0)
-        nc.gpsimd.tensor_tensor(out=kern_cost[:], in0=kern[:], in1=cost[:], op=ALU.mult)
+            nc.scalar.activation(out=cost[b][:], in_=sim[b][:], func=ACT.Copy, scale=-1.0, bias=1.0)
+            nc.gpsimd.tensor_tensor(out=kern_cost[b][:], in0=kern[b][:], in1=cost[b][:], op=ALU.mult)
 
-        u = small.tile([P, BATCH], F32, name="u0")
-        nc.vector.reciprocal(out=u[:], in_=row_sum[:])
-        for it in range(1, NUM_ITERS):
-            col_sum = psum.tile([P, BATCH], F32, tag="bank")
+        for it in range(NUM_ITERS):
+            if it > 0:
+                for b in range(BATCH):
+                    row_sum = psum.tile([P, 1], F32, tag="bank", name="row_sum%d" % b)
+                    nc.tensor.matmul(row_sum[:], lhsT=kern_t[b][:], rhs=v[b][:], start=True, stop=True)
+                    u[b] = turn.tile([P, 1], F32, name="u%d" % b)
+                    nc.vector.reciprocal(out=u[b][:], in_=row_sum[:])
             for b in range(BATCH):
-                nc.tensor.matmul(col_sum[:, b : b + 1], lhsT=kern[:, b, :], rhs=u[:, b : b + 1], start=True, stop=True)
-            v = small.tile([P, BATCH], F32, name="v%d" % it)
-            nc.vector.reciprocal(out=v[:], in_=col_sum[:])
-            row_sum_ps = psum.tile([P, BATCH], F32, tag="bank")
-            for b in range(BATCH):
-                nc.tensor.matmul(row_sum_ps[:, b : b + 1], lhsT=kern_t[:, b, :], rhs=v[:, b : b + 1], start=True, stop=True)
-            u = small.tile([P, BATCH], F32, name="u%d" % it)
-            nc.vector.reciprocal(out=u[:], in_=row_sum_ps[:])
+                col_sum = psum.tile([P, 1], F32, tag="bank", name="col_sum%d" % b)
+                nc.tensor.matmul(col_sum[:], lhsT=kern[b][:], rhs=u[b][:], start=True, stop=True)
+                v[b] = turn.tile([P, 1], F32, name="v%d" % b)
+                nc.vector.reciprocal(out=v[b][:], in_=col_sum[:])
 
-        col_sum_all = psum.tile([P, BATCH, P], F32, tag="bank")
-        cost_sum_all = psum.tile([P, BATCH, P], F32, tag="bank")
+        w = [small.tile([P, 1], F32, name="w%d" % b) for b in range(BATCH)]
         for b in range(BATCH):
-            u_all = u[:, b : b + 1].to_broadcast([P, P])
-            nc.tensor.matmul(col_sum_all[:, b, :], lhsT=u_all, rhs=kern[:, b, :], start=True, stop=True)
+            cost_sum = psum.tile([P, 1], F32, tag="bank", name="cost_sum%d" % b)
+            nc.tensor.matmul(cost_sum[:], lhsT=kern_cost[b][:], rhs=u[b][:], start=True, stop=True)
+            nc.scalar.copy(out=w[b][:], in_=cost_sum[:])
+
         for b in range(BATCH):
-            u_all = u[:, b : b + 1].to_broadcast([P, P])
-            nc.tensor.matmul(cost_sum_all[:, b, :], lhsT=u_all, rhs=kern_cost[:, b, :], start=True, stop=True)
-        v_all = small.tile([P, BATCH, P], F32)
-        nc.vector.reciprocal(out=v_all[:], in_=col_sum_all[:])
-        plan = small.tile([P, BATCH, P], F32)
-        for b in range(BATCH):
+            v_all = psum.tile([P, P], F32, tag="bank", name="v_all%d" % b)
+            nc.tensor.matmul(v_all[:], lhsT=v[b][:].to_broadcast([P, P]), rhs=identity[:], start=True, stop=True)
+            plan = small.tile([P, P], F32, name="plan%d" % b)
             nc.vector.scalar_tensor_tensor(
-                out=plan[:, b, :], in0=kern[:, b, :], scalar=u[:, b : b + 1], in1=v_all[:, b, :],
-                op0=ALU.mult, op1=ALU.mult,
+                out=plan[:], in0=kern[b][:], scalar=u[b][:], in1=v_all[:], op0=ALU.mult, op1=ALU.mult
             )
-        nc.sync.dma_start(out=out_0.rearrange("b i j -> i b j"), in_=plan[:])
-
-        terms = small.tile([P, BATCH, P], F32)
+            nc.sync.dma_start(out=out_0[b], in_=plan[:])
+        ot_sum = psum.tile([P, 1], F32, tag="bank")
+        for b in range(BATCH):
+            nc.tensor.matmul(
+                ot_sum[:], lhsT=w[b][:].to_broadcast([P, P]), rhs=v[b][:], start=(b == 0), stop=(b == BATCH - 1)
+            )
         ot_cost = small.tile([P, 1], F32)
-        nc.vector.scalar_tensor_tensor(
-            out=terms[:], in0=cost_sum_all[:], scalar=1.0 / BATCH, in1=v_all[:], op0=ALU.mult, op1=ALU.mult,
-            accum_out=ot_cost[:],
-        )
+        nc.vector.tensor_scalar_mul(out=ot_cost[:], in0=ot_sum[:], scalar1=1.0 / BATCH)
         ot_dst = out_1
         for missing in range(2 - out_1.ndim):
             ot_dst = ot_dst.unsqueeze(0)

@@ -31,12 +31,12 @@ FLOPS = 2 * (2 * BATCH * P * D * D) + 2 * BATCH * P * P * D
 
 
 def load_scale_planes(nc, planes, scales):
-    words = scales.bitcast(I32)
+    words = scales.bitcast(F32)
     for first in range(0, GROUPS, PLANES_PER_SLOT):
         count = min(PLANES_PER_SLOT, GROUPS - first)
         for quadrant in range(4):
-            nc.sync.dma_start(
-                out=planes[32 * quadrant : 32 * quadrant + 4 * count, first // PLANES_PER_SLOT, :].bitcast(I32),
+            nc.gpsimd.dma_start(
+                out=planes[32 * quadrant : 32 * quadrant + 4 * count, first // PLANES_PER_SLOT, :].bitcast(F32),
                 in_=words[first : first + count, 4 * quadrant : 4 * quadrant + 4, :],
             )
 
@@ -145,9 +145,9 @@ def tile_sinkhornot_w_kernel(
         planes_q = keep.tile([P, 2, D], U8, align_bytes=64)
         planes_k = keep.tile([P, 2, D], U8, align_bytes=64)
         bias_row = keep.tile([P, 2 * D], BF16)
-        nc.vector.memset(bias_row[:].bitcast(I32), 0)
         nc.vector.memset(planes_q[:].bitcast(I32), 0)
         nc.vector.memset(planes_k[:].bitcast(I32), 0)
+        nc.vector.memset(bias_row[:].bitcast(I32), 0)
         identity = const.tile([P, P], F32)
         make_identity(nc, identity[:])
         ones = const.tile([P, P], BF16)

@@ -108,6 +108,18 @@ def empty_range(nc, stage, acc, bias, y, sumsq, first):
             )
 
 
+def project(nc, psum, wpool, stage, weight, x_packed, bias, y, sumsq, between=None, after=None):
+    w_words, planes = weight
+    for first in range(0, D, RANGE):
+        acc = open_range(psum)
+        multiply_range(nc, wpool, acc, w_words, planes, x_packed, first)
+        if between and first == RANGE:
+            between()
+        empty_range(nc, stage, acc, bias, y, sumsq, first)
+        if after and first == RANGE:
+            after()
+
+
 def inverse_norms(nc, small, sumsq, minus_half, name):
     total = small.tile([P, BATCH], F32, name=name + "_total")
     nc.vector.tensor_reduce(out=total[:], in_=sumsq[:], axis=AXIS.X, op=ALU.add)
@@ -145,9 +157,10 @@ def tile_sinkhornot_w_kernel(
         planes_q = keep.tile([P, 2, D], U8, align_bytes=64)
         planes_k = keep.tile([P, 2, D], U8, align_bytes=64)
         bias_row = keep.tile([P, 2 * D], BF16)
+        nc.vector.memset(bias_row[:, 0:D].bitcast(I32), 0)
         nc.vector.memset(planes_q[:].bitcast(I32), 0)
+        nc.vector.memset(bias_row[:, D : 2 * D].bitcast(I32), 0)
         nc.vector.memset(planes_k[:].bitcast(I32), 0)
-        nc.vector.memset(bias_row[:].bitcast(I32), 0)
         identity = const.tile([P, P], F32)
         make_identity(nc, identity[:])
         ones = const.tile([P, P], BF16)
@@ -156,16 +169,17 @@ def tile_sinkhornot_w_kernel(
         nc.gpsimd.memset(minus_half[:], -0.5)
         warm = const.tile([P, 1], F32)
         nc.gpsimd.memset(warm[:], 0.0)
-        nc.scalar.activation(out=warm[:], in_=warm[:], func=ACT.Exp)
 
         drone = [rowpool.tile([P, D], BF16, tag="rows", name="drone%d" % b) for b in range(BATCH)]
         sat = [rowpool.tile([P, D], BF16, tag="rows", name="sat%d" % b) for b in range(BATCH)]
-        for b in range(BATCH):
-            nc.sync.dma_start(out=drone[b][:], in_=drone_tokens[b])
+        nc.scalar.dma_start(out=bias_row[0:1, 0:D], in_=bq.unsqueeze(0))
+        nc.scalar.dma_start(out=bias_row[0:1, D : 2 * D], in_=bk.unsqueeze(0))
+        nc.scalar.activation(out=warm[:], in_=warm[:], func=ACT.Exp)
+        for half in (slice(0, D // 2), slice(D // 2, D)):
+            for b in range(BATCH):
+                nc.sync.dma_start(out=drone[b][:, half], in_=drone_tokens[b][:, half])
         for b in range(BATCH):
             nc.sync.dma_start(out=sat[b][:], in_=sat_tokens[b])
-        nc.sync.dma_start(out=bias_row[0:1, 0:D], in_=bq.unsqueeze(0))
-        nc.sync.dma_start(out=bias_row[0:1, D : 2 * D], in_=bk.unsqueeze(0))
         load_scale_planes(nc, planes_q, Wq_scales)
         load_scale_planes(nc, planes_k, Wk_scales)
 
@@ -175,61 +189,61 @@ def tile_sinkhornot_w_kernel(
                 keep.tile([P, GROUPS, BATCH * P], U32, align_bytes=64, name=name + "_codes"),
                 keep.tile([P, GROUPS, BATCH * P], U8, align_bytes=64, name=name + "_scales"),
             )
-        copies = (nc.scalar.copy, nc.vector.tensor_copy)
-        for name, rows in (("drone", drone), ("sat", sat)):
-            grouped = {}
-            for g in range(GROUPS + QUANT_LAG):
-                if g < GROUPS:
-                    grouped[g] = flip_group(nc, psum, stage, identity, rows, every_second_word, g, copies[g % 2])
-                if g >= QUANT_LAG:
-                    quantise_group(nc, grouped[g - QUANT_LAG], g - QUANT_LAG, packed[name])
-
         bias = keep.tile([P, 2 * D], BF16)
-        for first in range(0, 2 * D, 2 * BANK):
-            spread = psum.tile([P, 2 * BANK], BF16, tag="bank")
-            for h in range(2):
-                nc.tensor.matmul(
-                    spread[:, BANK * h : BANK * (h + 1)], lhsT=ones[:],
-                    rhs=bias_row[:, first + BANK * h : first + BANK * (h + 1)], start=True, stop=True,
+        copies = (nc.scalar.copy, nc.vector.tensor_copy)
+        tokens_of = ((drone, packed["drone"]), (sat, packed["sat"]))
+        grouped = {}
+        for s in range(2 * GROUPS + QUANT_LAG):
+            if s < 2 * GROUPS:
+                grouped[s] = flip_group(
+                    nc, psum, stage, identity, tokens_of[s // GROUPS][0], every_second_word, s % GROUPS, copies[s % 2]
                 )
-            nc.scalar.copy(out=bias[:, first : first + 2 * BANK], in_=spread[:])
+                if s % 2 == 0:
+                    spread = psum.tile([P, 2 * BANK], BF16, tag="bank")
+                nc.tensor.matmul(
+                    spread[:, BANK * (s % 2) : BANK * (s % 2 + 1)], lhsT=ones[:],
+                    rhs=bias_row[:, BANK * s : BANK * (s + 1)], start=True, stop=True,
+                )
+                if s % 2 == 1:
+                    nc.scalar.copy(out=bias[:, BANK * (s - 1) : BANK * (s + 1)], in_=spread[:])
+            if s >= QUANT_LAG:
+                done = s - QUANT_LAG
+                quantise_group(nc, grouped[done], done % GROUPS, tokens_of[done // GROUPS][1])
 
         y_q = [ypool.tile([P, D], F32, tag="y", name="y_q%d" % b) for b in range(BATCH)]
         sumsq_q = small.tile([P, BATCH, D // BANK], F32)
-        for first in range(0, D, RANGE):
-            acc = open_range(psum)
-            multiply_range(nc, wpool, acc, Wq_words, planes_q, packed["drone"], first)
-            empty_range(nc, stage, acc, bias[:, 0:D], y_q, sumsq_q, first)
+        project(nc, psum, wpool, stage, (Wq_words, planes_q), packed["drone"], bias[:, 0:D], y_q, sumsq_q)
         inv_q = inverse_norms(nc, small, sumsq_q, minus_half, "q")
         q_rows = [rowpool.tile([P, D], BF16, tag="rows", name="q_rows%d" % b) for b in range(BATCH)]
         for g in range(GROUPS):
             normalise_group(nc, y_q, inv_q, q_rows, g)
 
+        q_grouped = {}
+
+        def flip_q():
+            for g in range(GROUPS):
+                q_grouped[g] = flip_group(nc, psum, stage, identity, q_rows, half_of_the_words, g, nc.scalar.copy)
+
+        def quantise_q():
+            for g in range(GROUPS):
+                quantise_group(nc, q_grouped[g], g, packed["q"])
+
         y_k = [ypool.tile([P, D], F32, tag="y", name="y_k%d" % b) for b in range(BATCH)]
         sumsq_k = small.tile([P, BATCH, D // BANK], F32)
-        for first in range(0, D, RANGE):
-            acc = open_range(psum)
-            multiply_range(nc, wpool, acc, Wk_words, planes_k, packed["sat"], first)
-            if first == RANGE:
-                grouped = [
-                    flip_group(nc, psum, stage, identity, q_rows, half_of_the_words, g, nc.scalar.copy)
-                    for g in range(GROUPS)
-                ]
-            empty_range(nc, stage, acc, bias[:, D : 2 * D], y_k, sumsq_k, first)
-            if first == RANGE:
-                for g in range(GROUPS):
-                    quantise_group(nc, grouped[g], g, packed["q"])
+        project(
+            nc, psum, wpool, stage, (Wk_words, planes_k), packed["sat"], bias[:, D : 2 * D], y_k, sumsq_k,
+            between=flip_q, after=quantise_q,
+        )
         inv_k = inverse_norms(nc, small, sumsq_k, minus_half, "k")
         k_rows = [rowpool.tile([P, D], BF16, tag="rows", name="k_rows%d" % b) for b in range(BATCH)]
         normalise_group(nc, y_k, inv_k, k_rows, GROUPS - 1, on_scalar=True)
         grouped = {}
-        for g in range(GROUPS + QUANT_LAG):
+        for g in range(GROUPS):
             if g < GROUPS - 1:
                 normalise_group(nc, y_k, inv_k, k_rows, g)
-            if g < GROUPS:
-                grouped[g] = flip_group(nc, psum, stage, identity, k_rows, half_of_the_words, g, nc.scalar.copy)
-            if g >= QUANT_LAG:
-                quantise_group(nc, grouped[g - QUANT_LAG], g - QUANT_LAG, packed["k"])
+            grouped[g] = flip_group(nc, psum, stage, identity, k_rows, half_of_the_words, g, nc.scalar.copy)
+        for g in range(GROUPS):
+            quantise_group(nc, grouped[g], g, packed["k"])
 
         sim = [psum.tile([P, P], F32, tag="bank", name="sim%d" % b) for b in range(BATCH)]
         sim_t = [psum.tile([P, P], F32, tag="bank", name="sim_t%d" % b) for b in range(BATCH)]

@@ -23,6 +23,7 @@ BANK = 512
 RANGE = 2 * BANK
 PLANES_PER_SLOT = 4
 QUANT_LAG = 2
+WARM_UPS = 5
 NUM_ITERS = 5
 INV_REG = 10.0
 EPS = 1e-12
@@ -31,12 +32,12 @@ FLOPS = 2 * (2 * BATCH * P * D * D) + 2 * BATCH * P * P * D
 
 
 def load_scale_planes(nc, planes, scales):
-    words = scales.bitcast(F32)
+    words = scales.bitcast(I32)
     for first in range(0, GROUPS, PLANES_PER_SLOT):
         count = min(PLANES_PER_SLOT, GROUPS - first)
         for quadrant in range(4):
-            nc.gpsimd.dma_start(
-                out=planes[32 * quadrant : 32 * quadrant + 4 * count, first // PLANES_PER_SLOT, :].bitcast(F32),
+            nc.sync.dma_start(
+                out=planes[32 * quadrant : 32 * quadrant + 4 * count, first // PLANES_PER_SLOT, :].bitcast(I32),
                 in_=words[first : first + count, 4 * quadrant : 4 * quadrant + 4, :],
             )
 
@@ -77,65 +78,118 @@ def open_range(psum):
     return [[psum.tile([P, BANK], F32, tag="bank", name="acc%d%d" % (b, h)) for h in range(2)] for b in range(BATCH)]
 
 
-def multiply_range(nc, wpool, acc, w_words, planes, x_packed, first):
+def load_range(nc, wpool, w_words, first):
     words = w_words.rearrange("g p n t -> g p (n t)").bitcast(I32)
-    x_codes, x_scales = x_packed
+    chunks = []
     for g in range(GROUPS):
-        chunk = wpool.tile([P, RANGE], U32, align_bytes=64)
+        chunk = wpool.tile([P, RANGE], U32, align_bytes=64, tag="chunk", name="chunk%d" % g)
         nc.sync.dma_start(out=chunk[:].bitcast(I32), in_=words[g, :, first : first + RANGE])
+        chunks.append(chunk)
+    return chunks
+
+
+def multiply_pass(nc, acc, chunk, planes, x_packed, b, g, first, start, width):
+    x_codes, x_scales = x_packed
+    nc.tensor.matmul_mx(
+        out=acc[:],
+        lhsT=x_codes[:, g, P * b : P * (b + 1)].bitcast(FP8X4),
+        lhsT_scale=x_scales[:, g, P * b : P * (b + 1)],
+        rhs=chunk[:, start - first : start - first + width].bitcast(FP8X4),
+        rhs_scale=scale_plane(planes, g, slice(start, start + width)),
+        start=(g == 0),
+        stop=(g == GROUPS - 1),
+    )
+
+
+def multiply_range(nc, acc, chunks, planes, x_packed, first):
+    for g in range(GROUPS):
         for b in range(BATCH):
             for h in range(2):
-                nc.tensor.matmul_mx(
-                    out=acc[b][h][:],
-                    lhsT=x_codes[:, g, P * b : P * (b + 1)].bitcast(FP8X4),
-                    lhsT_scale=x_scales[:, g, P * b : P * (b + 1)],
-                    rhs=chunk[:, BANK * h : BANK * (h + 1)].bitcast(FP8X4),
-                    rhs_scale=scale_plane(planes, g, slice(first + BANK * h, first + BANK * (h + 1))),
-                    start=(g == 0),
-                    stop=(g == GROUPS - 1),
-                )
+                multiply_pass(nc, acc[b][h], chunks[g], planes, x_packed, b, g, first, first + BANK * h, BANK)
 
 
-def empty_range(nc, stage, acc, bias, y, sumsq, first):
+def add_bias(nc, acc, bias, y, start, width):
+    cols = slice(start, start + width)
+    nc.vector.tensor_tensor(out=y[:, cols], in0=acc[:], in1=bias[:, cols], op=ALU.add)
+
+
+def sum_squares(nc, junk, y, square_sum, start, width):
+    squares = junk.tile([P, BANK], BF16)
+    nc.scalar.activation(
+        out=squares[:, 0:width], in_=y[:, start : start + width], func=ACT.Square, accum_out=square_sum
+    )
+
+
+def add_bias_range(nc, acc, bias, y, first):
     for b in range(BATCH):
         for h in range(2):
-            cols = slice(first + BANK * h, first + BANK * (h + 1))
-            nc.vector.tensor_tensor(out=y[b][:, cols], in0=acc[b][h][:], in1=bias[:, cols], op=ALU.add)
-            squares = stage.tile([P, BANK], BF16)
-            block = (first + BANK * h) // BANK
-            nc.scalar.activation(
-                out=squares[:], in_=y[b][:, cols], func=ACT.Square, accum_out=sumsq[:, b, block : block + 1]
-            )
+            add_bias(nc, acc[b][h], bias, y[b], first + BANK * h, BANK)
 
 
-def project(nc, psum, wpool, stage, weight, x_packed, bias, y, sumsq, between=None, after=None):
-    w_words, planes = weight
-    for first in range(0, D, RANGE):
-        acc = open_range(psum)
-        multiply_range(nc, wpool, acc, w_words, planes, x_packed, first)
-        if between and first == RANGE:
-            between()
-        empty_range(nc, stage, acc, bias, y, sumsq, first)
-        if after and first == RANGE:
-            after()
+def sum_squares_range(nc, junk, y, sumsq, first):
+    for b in range(BATCH):
+        for h in range(2):
+            block = first // BANK + h
+            sum_squares(nc, junk, y[b], sumsq[:, b, block : block + 1], first + BANK * h, BANK)
 
 
-def inverse_norms(nc, small, sumsq, minus_half, name):
-    total = small.tile([P, BATCH], F32, name=name + "_total")
-    nc.vector.tensor_reduce(out=total[:], in_=sumsq[:], axis=AXIS.X, op=ALU.add)
-    nc.vector.tensor_scalar_max(out=total[:], in0=total[:], scalar1=EPS * EPS)
-    inv = small.tile([P, BATCH], F32, name=name + "_inv")
+def inverse_norm(nc, small, sumsq, b, minus_half, name):
+    last = sumsq.shape[2] - 1
+    partial = small.tile([P, 1], F32, name=name + "_partial")
+    nc.vector.tensor_reduce(out=partial[:], in_=sumsq[:, b, 0:last], axis=AXIS.X, op=ALU.add)
+    total = small.tile([P, 1], F32, name=name + "_total")
+    nc.gpsimd.tensor_scalar(
+        out=total[:], in0=sumsq[:, b, last : last + 1], scalar1=partial[:], scalar2=EPS * EPS, op0=ALU.add, op1=ALU.max
+    )
+    inv = small.tile([P, 1], F32, name=name + "_inv")
     nc.gpsimd.tensor_tensor(out=inv[:], in0=total[:], in1=minus_half[:], op=ALU.pow)
     return inv
 
 
 def normalise_group(nc, y, inv, rows, g, on_scalar=False):
     cols = slice(K_PASS * g, K_PASS * (g + 1))
-    for b in range(BATCH):
-        if on_scalar:
-            nc.scalar.activation(out=rows[b][:, cols], in_=y[b][:, cols], func=ACT.Copy, scale=inv[:, b : b + 1])
-        else:
-            nc.vector.tensor_scalar_mul(out=rows[b][:, cols], in0=y[b][:, cols], scalar1=inv[:, b : b + 1])
+    if on_scalar:
+        nc.scalar.activation(out=rows[:, cols], in_=y[:, cols], func=ACT.Copy, scale=inv[:])
+    else:
+        nc.vector.tensor_scalar_mul(out=rows[:, cols], in0=y[:, cols], scalar1=inv[:])
+
+
+def flip_rows(nc, psum, stage, identity, rows, g, copy):
+    words = rows[:].bitcast(F32)
+    flipped = psum.tile([P, 2, P], F32, tag="bank", name="flipped_rows")
+    for u in range(2):
+        nc.tensor.transpose(flipped[:, u, :], words[:, half_of_the_words(g, u)], identity[:])
+    grouped = stage.tile([P, P, 2], F32, align_bytes=64, tag="grouped_rows", name="grouped_rows")
+    copy(out=grouped[:], in_=flipped[:].rearrange("p u r -> p r u"))
+    return grouped
+
+
+def quantise_rows(nc, grouped, g, b, packed):
+    codes, scales = packed
+    tokens = slice(P * b, P * (b + 1))
+    nc.vector.quantize_mx(
+        out=codes[:, g, tokens].bitcast(FP8X4),
+        scales=scales[:, g, tokens],
+        in_=grouped[:].rearrange("p r u -> p (r u)").bitcast(BF16),
+    )
+
+
+def multiply_sim(nc, psum, packed, b):
+    sim = psum.tile([P, P], F32, tag="bank", name="sim%d" % b)
+    sim_t = psum.tile([P, P], F32, tag="bank", name="sim_t%d" % b)
+    tokens = slice(P * b, P * (b + 1))
+    for g in range(GROUPS):
+        for out, left, right in ((sim, "q", "k"), (sim_t, "k", "q")):
+            nc.tensor.matmul_mx(
+                out=out[:],
+                lhsT=packed[left][0][:, g, tokens].bitcast(FP8X4),
+                lhsT_scale=packed[left][1][:, g, tokens],
+                rhs=packed[right][0][:, g, tokens].bitcast(FP8X4),
+                rhs_scale=packed[right][1][:, g, tokens],
+                start=(g == 0),
+                stop=(g == GROUPS - 1),
+            )
+    return sim, sim_t
 
 
 def tile_sinkhornot_w_kernel(
@@ -149,8 +203,9 @@ def tile_sinkhornot_w_kernel(
         turn = ctx.enter_context(tc.tile_pool(name="turn", bufs=2))
         rowpool = ctx.enter_context(tc.tile_pool(name="rowpool", bufs=4))
         ypool = ctx.enter_context(tc.tile_pool(name="ypool", bufs=4))
-        wpool = ctx.enter_context(tc.tile_pool(name="wpool", bufs=12))
+        wpool = ctx.enter_context(tc.tile_pool(name="wpool", bufs=16))
         stage = ctx.enter_context(tc.tile_pool(name="stage", bufs=GROUPS))
+        junk = ctx.enter_context(tc.tile_pool(name="junk", bufs=2))
         psum = ctx.enter_context(tc.psum_pool(name="psum", bufs=8))
         ctx.enter_context(tc.manual_schedule())
 
@@ -159,13 +214,11 @@ def tile_sinkhornot_w_kernel(
         bias_row = keep.tile([P, 2 * D], BF16)
         nc.vector.memset(bias_row[:, 0:D].bitcast(I32), 0)
         nc.vector.memset(planes_q[:].bitcast(I32), 0)
-        nc.vector.memset(bias_row[:, D : 2 * D].bitcast(I32), 0)
-        nc.vector.memset(planes_k[:].bitcast(I32), 0)
         identity = const.tile([P, P], F32)
         make_identity(nc, identity[:])
-        ones = const.tile([P, P], BF16)
+        ones = const.tile([P, BANK], BF16)
         nc.gpsimd.memset(ones[:], 1.0)
-        minus_half = const.tile([P, BATCH], F32)
+        minus_half = const.tile([P, 1], F32)
         nc.gpsimd.memset(minus_half[:], -0.5)
         warm = const.tile([P, 1], F32)
         nc.gpsimd.memset(warm[:], 0.0)
@@ -173,15 +226,11 @@ def tile_sinkhornot_w_kernel(
         drone = [rowpool.tile([P, D], BF16, tag="rows", name="drone%d" % b) for b in range(BATCH)]
         sat = [rowpool.tile([P, D], BF16, tag="rows", name="sat%d" % b) for b in range(BATCH)]
         nc.scalar.dma_start(out=bias_row[0:1, 0:D], in_=bq.unsqueeze(0))
-        nc.scalar.dma_start(out=bias_row[0:1, D : 2 * D], in_=bk.unsqueeze(0))
         nc.scalar.activation(out=warm[:], in_=warm[:], func=ACT.Exp)
         for half in (slice(0, D // 2), slice(D // 2, D)):
             for b in range(BATCH):
                 nc.sync.dma_start(out=drone[b][:, half], in_=drone_tokens[b][:, half])
-        for b in range(BATCH):
-            nc.sync.dma_start(out=sat[b][:], in_=sat_tokens[b])
         load_scale_planes(nc, planes_q, Wq_scales)
-        load_scale_planes(nc, planes_k, Wk_scales)
 
         packed = {}
         for name in ("drone", "sat", "q", "k"):
@@ -190,76 +239,102 @@ def tile_sinkhornot_w_kernel(
                 keep.tile([P, GROUPS, BATCH * P], U8, align_bytes=64, name=name + "_scales"),
             )
         bias = keep.tile([P, 2 * D], BF16)
-        copies = (nc.scalar.copy, nc.vector.tensor_copy)
-        tokens_of = ((drone, packed["drone"]), (sat, packed["sat"]))
         grouped = {}
-        for s in range(2 * GROUPS + QUANT_LAG):
-            if s < 2 * GROUPS:
-                grouped[s] = flip_group(
-                    nc, psum, stage, identity, tokens_of[s // GROUPS][0], every_second_word, s % GROUPS, copies[s % 2]
-                )
-                if s % 2 == 0:
-                    spread = psum.tile([P, 2 * BANK], BF16, tag="bank")
-                nc.tensor.matmul(
-                    spread[:, BANK * (s % 2) : BANK * (s % 2 + 1)], lhsT=ones[:],
-                    rhs=bias_row[:, BANK * s : BANK * (s + 1)], start=True, stop=True,
-                )
-                if s % 2 == 1:
-                    nc.scalar.copy(out=bias[:, BANK * (s - 1) : BANK * (s + 1)], in_=spread[:])
+
+        def spread_bias(block, copy):
+            cols = slice(BANK * block, BANK * (block + 1))
+            spread = psum.tile([P, BANK], BF16, tag="bank", name="spread")
+            nc.tensor.matmul(spread[:], lhsT=ones[:, 0:P], rhs=bias_row[:, cols], start=True, stop=True)
+            copy(out=bias[:, cols], in_=spread[:])
+
+        for i in range(WARM_UPS):
+            dummy = psum.tile([P, BANK], F32, tag="bank", name="dummy")
+            nc.tensor.matmul(dummy[:], lhsT=ones[:, 0:P], rhs=ones[:], start=True, stop=True)
+        for s in range(GROUPS + QUANT_LAG):
+            if s < GROUPS:
+                copy = (nc.scalar.copy, nc.vector.tensor_copy)[s % 2]
+                grouped[s] = flip_group(nc, psum, stage, identity, drone, every_second_word, s, copy)
+                if s >= GROUPS // 2:
+                    for block in (2 * s - GROUPS, 2 * s - GROUPS + 1):
+                        spread_bias(block, nc.scalar.copy)
             if s >= QUANT_LAG:
-                done = s - QUANT_LAG
-                quantise_group(nc, grouped[done], done % GROUPS, tokens_of[done // GROUPS][1])
+                quantise_group(nc, grouped[s - QUANT_LAG], s - QUANT_LAG, packed["drone"])
+
+        nc.vector.memset(bias_row[:, D : 2 * D].bitcast(I32), 0)
+        nc.vector.memset(planes_k[:].bitcast(I32), 0)
+        nc.scalar.dma_start(out=bias_row[0:1, D : 2 * D], in_=bk.unsqueeze(0))
 
         y_q = [ypool.tile([P, D], F32, tag="y", name="y_q%d" % b) for b in range(BATCH)]
         sumsq_q = small.tile([P, BATCH, D // BANK], F32)
-        project(nc, psum, wpool, stage, (Wq_words, planes_q), packed["drone"], bias[:, 0:D], y_q, sumsq_q)
-        inv_q = inverse_norms(nc, small, sumsq_q, minus_half, "q")
+        for first in range(0, D, RANGE):
+            acc = open_range(psum)
+            chunks = load_range(nc, wpool, Wq_words, first)
+            if first == 0:
+                for b in range(BATCH):
+                    nc.sync.dma_start(out=sat[b][:], in_=sat_tokens[b])
+            multiply_range(nc, acc, chunks, planes_q, packed["drone"], first)
+            add_bias_range(nc, acc, bias[:, 0:D], y_q, first)
+            groups = range(3 * (first // RANGE), 3 * (first // RANGE) + 3) if first < 2 * RANGE else ()
+            for g in groups:
+                grouped[g] = flip_group(nc, psum, stage, identity, sat, every_second_word, g, nc.scalar.copy)
+                spread_bias(GROUPS + g, nc.vector.tensor_copy)
+            for g in groups:
+                quantise_group(nc, grouped[g], g, packed["sat"])
+            sum_squares_range(nc, junk, y_q, sumsq_q, first)
+        load_scale_planes(nc, planes_k, Wk_scales)
         q_rows = [rowpool.tile([P, D], BF16, tag="rows", name="q_rows%d" % b) for b in range(BATCH)]
-        for g in range(GROUPS):
-            normalise_group(nc, y_q, inv_q, q_rows, g)
-
-        q_grouped = {}
-
-        def flip_q():
-            for g in range(GROUPS):
-                q_grouped[g] = flip_group(nc, psum, stage, identity, q_rows, half_of_the_words, g, nc.scalar.copy)
-
-        def quantise_q():
-            for g in range(GROUPS):
-                quantise_group(nc, q_grouped[g], g, packed["q"])
-
-        y_k = [ypool.tile([P, D], F32, tag="y", name="y_k%d" % b) for b in range(BATCH)]
-        sumsq_k = small.tile([P, BATCH, D // BANK], F32)
-        project(
-            nc, psum, wpool, stage, (Wk_words, planes_k), packed["sat"], bias[:, D : 2 * D], y_k, sumsq_k,
-            between=flip_q, after=quantise_q,
-        )
-        inv_k = inverse_norms(nc, small, sumsq_k, minus_half, "k")
-        k_rows = [rowpool.tile([P, D], BF16, tag="rows", name="k_rows%d" % b) for b in range(BATCH)]
-        normalise_group(nc, y_k, inv_k, k_rows, GROUPS - 1, on_scalar=True)
-        grouped = {}
-        for g in range(GROUPS):
-            if g < GROUPS - 1:
-                normalise_group(nc, y_k, inv_k, k_rows, g)
-            grouped[g] = flip_group(nc, psum, stage, identity, k_rows, half_of_the_words, g, nc.scalar.copy)
-        for g in range(GROUPS):
-            quantise_group(nc, grouped[g], g, packed["k"])
-
-        sim = [psum.tile([P, P], F32, tag="bank", name="sim%d" % b) for b in range(BATCH)]
-        sim_t = [psum.tile([P, P], F32, tag="bank", name="sim_t%d" % b) for b in range(BATCH)]
+        inv_q = [inverse_norm(nc, small, sumsq_q, b, minus_half, "q%d" % b) for b in range(BATCH)]
         for g in range(GROUPS):
             for b in range(BATCH):
-                tokens = slice(P * b, P * (b + 1))
-                for out, left, right in ((sim[b], "q", "k"), (sim_t[b], "k", "q")):
-                    nc.tensor.matmul_mx(
-                        out=out[:],
-                        lhsT=packed[left][0][:, g, tokens].bitcast(FP8X4),
-                        lhsT_scale=packed[left][1][:, g, tokens],
-                        rhs=packed[right][0][:, g, tokens].bitcast(FP8X4),
-                        rhs_scale=packed[right][1][:, g, tokens],
-                        start=(g == 0),
-                        stop=(g == GROUPS - 1),
-                    )
+                normalise_group(nc, y_q[b], inv_q[b], q_rows[b], g)
+
+        y_k = [ypool.tile([P, D], F32, tag="y", name="y_k%d" % b) for b in range(BATCH)]
+        sumsq_k = small.tile([P, BATCH, D // BANK + 1], F32)
+        bias_k = bias[:, D : 2 * D]
+        q_grouped = {}
+        for first in (0, RANGE):
+            acc = open_range(psum)
+            chunks = load_range(nc, wpool, Wk_words, first)
+            multiply_range(nc, acc, chunks, planes_k, packed["sat"], first)
+            add_bias_range(nc, acc, bias_k, y_k, first)
+            if first == RANGE:
+                for g in range(GROUPS):
+                    q_grouped[g] = flip_group(nc, psum, stage, identity, q_rows, half_of_the_words, g, nc.scalar.copy)
+            sum_squares_range(nc, junk, y_k, sumsq_k, first)
+        last_range = 2 * RANGE
+        chunks = load_range(nc, wpool, Wk_words, last_range)
+        k_rows = [rowpool.tile([P, D], BF16, tag="rows", name="k_rows%d" % b) for b in range(BATCH)]
+        pieces = [(last_range, BANK), (last_range + BANK, BANK // 2), (last_range + 3 * BANK // 2, BANK // 2)]
+        k_grouped = {}
+        inv_k = {}
+        for b in range(BATCH):
+            for i, (start, width) in enumerate(pieces):
+                piece = psum.tile([P, width], F32, tag="bank", name="piece")
+                for g in range(GROUPS):
+                    multiply_pass(nc, piece, chunks[g], planes_k, packed["sat"], b, g, last_range, start, width)
+                square_sum = sumsq_k[:, b, 4 + i : 5 + i]
+                add_bias(nc, piece, bias_k, y_k[b], start, width)
+                sum_squares(nc, junk, y_k[b], square_sum, start, width)
+                if b == 0 and i == 0:
+                    for g in range(GROUPS):
+                        quantise_group(nc, q_grouped[g], g, packed["q"])
+                if b == 1 and i == 0:
+                    for g in range(GROUPS):
+                        normalise_group(nc, y_k[0], inv_k[0], k_rows[0], g)
+            inv_k[b] = inverse_norm(nc, small, sumsq_k, b, minus_half, "k%d" % b)
+        for g in range(GROUPS):
+            copy = nc.vector.tensor_copy if g < GROUPS // 2 else nc.scalar.copy
+            k_grouped[g] = flip_rows(nc, psum, stage, identity, k_rows[0], g, copy)
+        for g in range(GROUPS):
+            quantise_rows(nc, k_grouped[g], g, 0, packed["k"])
+        sims = {0: multiply_sim(nc, psum, packed, 0)}
+        normalise_group(nc, y_k[1], inv_k[1], k_rows[1], GROUPS - 1, on_scalar=True)
+        for g in range(GROUPS):
+            if g < GROUPS - 1:
+                normalise_group(nc, y_k[1], inv_k[1], k_rows[1], g)
+            k_grouped[g] = flip_rows(nc, psum, stage, identity, k_rows[1], g, nc.scalar.copy)
+        for g in range(GROUPS):
+            quantise_rows(nc, k_grouped[g], g, 1, packed["k"])
 
         kern = [small.tile([P, P], F32, name="kern%d" % b) for b in range(BATCH)]
         kern_t = [small.tile([P, P], F32, name="kern_t%d" % b) for b in range(BATCH)]
@@ -268,16 +343,17 @@ def tile_sinkhornot_w_kernel(
         u = [None, None]
         v = [None, None]
         for b in range(BATCH):
+            if b == 1:
+                sims[1] = multiply_sim(nc, psum, packed, 1)
+            sim, sim_t = sims[b]
             row_sum = turn.tile([P, 1], F32, name="first_row_sum%d" % b)
             nc.scalar.activation(
-                out=kern[b][:], in_=sim[b][:], func=ACT.Exp, scale=INV_REG, bias=-INV_REG, accum_out=row_sum[:]
+                out=kern[b][:], in_=sim[:], func=ACT.Exp, scale=INV_REG, bias=-INV_REG, accum_out=row_sum[:]
             )
             u[b] = turn.tile([P, 1], F32, name="u%d" % b)
             nc.vector.reciprocal(out=u[b][:], in_=row_sum[:])
-        for b in range(BATCH):
-            nc.scalar.activation(out=kern_t[b][:], in_=sim_t[b][:], func=ACT.Exp, scale=INV_REG, bias=-INV_REG)
-        for b in range(BATCH):
-            nc.scalar.activation(out=cost[b][:], in_=sim[b][:], func=ACT.Copy, scale=-1.0, bias=1.0)
+            nc.scalar.activation(out=kern_t[b][:], in_=sim_t[:], func=ACT.Exp, scale=INV_REG, bias=-INV_REG)
+            nc.scalar.activation(out=cost[b][:], in_=sim[:], func=ACT.Copy, scale=-1.0, bias=1.0)
             nc.gpsimd.tensor_tensor(out=kern_cost[b][:], in0=kern[b][:], in1=cost[b][:], op=ALU.mult)
 
         for it in range(NUM_ITERS):

@@ -32,12 +32,12 @@ FLOPS = 2 * (2 * BATCH * P * D * D) + 2 * BATCH * P * P * D
 
 
 def load_scale_planes(nc, planes, scales):
-    words = scales.bitcast(I32)
+    words = scales.bitcast(F32)
     for first in range(0, GROUPS, PLANES_PER_SLOT):
         count = min(PLANES_PER_SLOT, GROUPS - first)
         for quadrant in range(4):
-            nc.sync.dma_start(
-                out=planes[32 * quadrant : 32 * quadrant + 4 * count, first // PLANES_PER_SLOT, :].bitcast(I32),
+            nc.scalar.dma_start(
+                out=planes[32 * quadrant : 32 * quadrant + 4 * count, first // PLANES_PER_SLOT, :].bitcast(F32),
                 in_=words[first : first + count, 4 * quadrant : 4 * quadrant + 4, :],
             )
 
@@ -212,8 +212,8 @@ def tile_sinkhornot_w_kernel(
         planes_q = keep.tile([P, 2, D], U8, align_bytes=64)
         planes_k = keep.tile([P, 2, D], U8, align_bytes=64)
         bias_row = keep.tile([P, 2 * D], BF16)
-        nc.vector.memset(bias_row[:, 0:D].bitcast(I32), 0)
         nc.vector.memset(planes_q[:].bitcast(I32), 0)
+        nc.vector.memset(bias_row[:, 0:D].bitcast(I32), 0)
         identity = const.tile([P, P], F32)
         make_identity(nc, identity[:])
         ones = const.tile([P, BANK], BF16)
@@ -225,12 +225,12 @@ def tile_sinkhornot_w_kernel(
 
         drone = [rowpool.tile([P, D], BF16, tag="rows", name="drone%d" % b) for b in range(BATCH)]
         sat = [rowpool.tile([P, D], BF16, tag="rows", name="sat%d" % b) for b in range(BATCH)]
-        nc.scalar.dma_start(out=bias_row[0:1, 0:D], in_=bq.unsqueeze(0))
         nc.scalar.activation(out=warm[:], in_=warm[:], func=ACT.Exp)
+        load_scale_planes(nc, planes_q, Wq_scales)
+        nc.scalar.dma_start(out=bias_row[0:1, 0:D], in_=bq.unsqueeze(0))
         for half in (slice(0, D // 2), slice(D // 2, D)):
             for b in range(BATCH):
                 nc.sync.dma_start(out=drone[b][:, half], in_=drone_tokens[b][:, half])
-        load_scale_planes(nc, planes_q, Wq_scales)
 
         packed = {}
         for name in ("drone", "sat", "q", "k"):
@@ -263,6 +263,7 @@ def tile_sinkhornot_w_kernel(
         nc.vector.memset(bias_row[:, D : 2 * D].bitcast(I32), 0)
         nc.vector.memset(planes_k[:].bitcast(I32), 0)
         nc.scalar.dma_start(out=bias_row[0:1, D : 2 * D], in_=bk.unsqueeze(0))
+        load_scale_planes(nc, planes_k, Wk_scales)
 
         y_q = [ypool.tile([P, D], F32, tag="y", name="y_q%d" % b) for b in range(BATCH)]
         sumsq_q = small.tile([P, BATCH, D // BANK], F32)
@@ -281,7 +282,6 @@ def tile_sinkhornot_w_kernel(
             for g in groups:
                 quantise_group(nc, grouped[g], g, packed["sat"])
             sum_squares_range(nc, junk, y_q, sumsq_q, first)
-        load_scale_planes(nc, planes_k, Wk_scales)
         q_rows = [rowpool.tile([P, D], BF16, tag="rows", name="q_rows%d" % b) for b in range(BATCH)]
         inv_q = [inverse_norm(nc, small, sumsq_q, b, minus_half, "q%d" % b) for b in range(BATCH)]
         for g in range(GROUPS):

@@ -36,7 +36,7 @@ def load_scale_planes(nc, planes, scales):
     for first in range(0, GROUPS, PLANES_PER_SLOT):
         count = min(PLANES_PER_SLOT, GROUPS - first)
         for quadrant in range(4):
-            nc.scalar.dma_start(
+            nc.gpsimd.dma_start(
                 out=planes[32 * quadrant : 32 * quadrant + 4 * count, first // PLANES_PER_SLOT, :].bitcast(F32),
                 in_=words[first : first + count, 4 * quadrant : 4 * quadrant + 4, :],
             )

@@ -31,13 +31,13 @@ EPS = 1e-12
 FLOPS = 2 * (2 * BATCH * P * D * D) + 2 * BATCH * P * P * D
 
 
-def load_scale_planes(nc, planes, scales):
-    words = scales.bitcast(F32)
+def load_scale_planes(load, planes, scales, dtype):
+    words = scales.bitcast(dtype)
     for first in range(0, GROUPS, PLANES_PER_SLOT):
         count = min(PLANES_PER_SLOT, GROUPS - first)
         for quadrant in range(4):
-            nc.gpsimd.dma_start(
-                out=planes[32 * quadrant : 32 * quadrant + 4 * count, first // PLANES_PER_SLOT, :].bitcast(F32),
+            load(
+                out=planes[32 * quadrant : 32 * quadrant + 4 * count, first // PLANES_PER_SLOT, :].bitcast(dtype),
                 in_=words[first : first + count, 4 * quadrant : 4 * quadrant + 4, :],
             )
 
@@ -101,8 +101,10 @@ def multiply_pass(nc, acc, chunk, planes, x_packed, b, g, first, start, width):
     )
 
 
-def multiply_range(nc, acc, chunks, planes, x_packed, first):
+def multiply_range(nc, acc, chunks, planes, x_packed, first, halfway=None):
     for g in range(GROUPS):
+        if halfway and g == GROUPS // 2:
+            halfway()
         for b in range(BATCH):
             for h in range(2):
                 multiply_pass(nc, acc[b][h], chunks[g], planes, x_packed, b, g, first, first + BANK * h, BANK)
@@ -133,21 +135,21 @@ def sum_squares_range(nc, junk, y, sumsq, first):
             sum_squares(nc, junk, y[b], sumsq[:, b, block : block + 1], first + BANK * h, BANK)
 
 
-def inverse_norm(nc, small, sumsq, b, minus_half, name):
-    last = sumsq.shape[2] - 1
+def inverse_norm(nc, small, sums, minus_half, name):
+    last = sums.shape[1] - 1
     partial = small.tile([P, 1], F32, name=name + "_partial")
-    nc.vector.tensor_reduce(out=partial[:], in_=sumsq[:, b, 0:last], axis=AXIS.X, op=ALU.add)
+    nc.vector.tensor_reduce(out=partial[:], in_=sums[:, 0:last], axis=AXIS.X, op=ALU.add)
     total = small.tile([P, 1], F32, name=name + "_total")
     nc.gpsimd.tensor_scalar(
-        out=total[:], in0=sumsq[:, b, last : last + 1], scalar1=partial[:], scalar2=EPS * EPS, op0=ALU.add, op1=ALU.max
+        out=total[:], in0=sums[:, last : last + 1], scalar1=partial[:], scalar2=EPS * EPS, op0=ALU.add, op1=ALU.max
     )
     inv = small.tile([P, 1], F32, name=name + "_inv")
     nc.gpsimd.tensor_tensor(out=inv[:], in0=total[:], in1=minus_half[:], op=ALU.pow)
     return inv
 
 
-def normalise_group(nc, y, inv, rows, g, on_scalar=False):
-    cols = slice(K_PASS * g, K_PASS * (g + 1))
+def normalise(nc, y, inv, rows, first, count=1, on_scalar=False):
+    cols = slice(K_PASS * first, K_PASS * (first + count))
     if on_scalar:
         nc.scalar.activation(out=rows[:, cols], in_=y[:, cols], func=ACT.Copy, scale=inv[:])
     else:
@@ -212,8 +214,8 @@ def tile_sinkhornot_w_kernel(
         planes_q = keep.tile([P, 2, D], U8, align_bytes=64)
         planes_k = keep.tile([P, 2, D], U8, align_bytes=64)
         bias_row = keep.tile([P, 2 * D], BF16)
-        nc.vector.memset(planes_q[:].bitcast(I32), 0)
         nc.vector.memset(bias_row[:, 0:D].bitcast(I32), 0)
+        nc.vector.memset(planes_q[:].bitcast(I32), 0)
         identity = const.tile([P, P], F32)
         make_identity(nc, identity[:])
         ones = const.tile([P, BANK], BF16)
@@ -226,11 +228,11 @@ def tile_sinkhornot_w_kernel(
         drone = [rowpool.tile([P, D], BF16, tag="rows", name="drone%d" % b) for b in range(BATCH)]
         sat = [rowpool.tile([P, D], BF16, tag="rows", name="sat%d" % b) for b in range(BATCH)]
         nc.scalar.activation(out=warm[:], in_=warm[:], func=ACT.Exp)
-        load_scale_planes(nc, planes_q, Wq_scales)
         nc.scalar.dma_start(out=bias_row[0:1, 0:D], in_=bq.unsqueeze(0))
         for half in (slice(0, D // 2), slice(D // 2, D)):
             for b in range(BATCH):
                 nc.sync.dma_start(out=drone[b][:, half], in_=drone_tokens[b][:, half])
+        load_scale_planes(nc.sync.dma_start, planes_q, Wq_scales, I32)
 
         packed = {}
         for name in ("drone", "sat", "q", "k"):
@@ -247,6 +249,10 @@ def tile_sinkhornot_w_kernel(
             nc.tensor.matmul(spread[:], lhsT=ones[:, 0:P], rhs=bias_row[:, cols], start=True, stop=True)
             copy(out=bias[:, cols], in_=spread[:])
 
+        def spread_bq():
+            for block in range(GROUPS):
+                spread_bias(block, nc.scalar.copy)
+
         for i in range(WARM_UPS):
             dummy = psum.tile([P, BANK], F32, tag="bank", name="dummy")
             nc.tensor.matmul(dummy[:], lhsT=ones[:, 0:P], rhs=ones[:], start=True, stop=True)
@@ -254,16 +260,13 @@ def tile_sinkhornot_w_kernel(
             if s < GROUPS:
                 copy = (nc.scalar.copy, nc.vector.tensor_copy)[s % 2]
                 grouped[s] = flip_group(nc, psum, stage, identity, drone, every_second_word, s, copy)
-                if s >= GROUPS // 2:
-                    for block in (2 * s - GROUPS, 2 * s - GROUPS + 1):
-                        spread_bias(block, nc.scalar.copy)
             if s >= QUANT_LAG:
                 quantise_group(nc, grouped[s - QUANT_LAG], s - QUANT_LAG, packed["drone"])
 
         nc.vector.memset(bias_row[:, D : 2 * D].bitcast(I32), 0)
-        nc.vector.memset(planes_k[:].bitcast(I32), 0)
         nc.scalar.dma_start(out=bias_row[0:1, D : 2 * D], in_=bk.unsqueeze(0))
-        load_scale_planes(nc, planes_k, Wk_scales)
+        nc.vector.memset(planes_k[:].bitcast(I32), 0)
+        load_scale_planes(nc.gpsimd.dma_start, planes_k, Wk_scales, F32)
 
         y_q = [ypool.tile([P, D], F32, tag="y", name="y_q%d" % b) for b in range(BATCH)]
         sumsq_q = small.tile([P, BATCH, D // BANK], F32)
@@ -273,65 +276,98 @@ def tile_sinkhornot_w_kernel(
             if first == 0:
                 for b in range(BATCH):
                     nc.sync.dma_start(out=sat[b][:], in_=sat_tokens[b])
-            multiply_range(nc, acc, chunks, planes_q, packed["drone"], first)
+            multiply_range(
+                nc, acc, chunks, planes_q, packed["drone"], first, halfway=spread_bq if first == 0 else None
+            )
             add_bias_range(nc, acc, bias[:, 0:D], y_q, first)
             groups = range(3 * (first // RANGE), 3 * (first // RANGE) + 3) if first < 2 * RANGE else ()
             for g in groups:
                 grouped[g] = flip_group(nc, psum, stage, identity, sat, every_second_word, g, nc.scalar.copy)
-                spread_bias(GROUPS + g, nc.vector.tensor_copy)
+            if first == RANGE:
+                for block in range(GROUPS, 2 * GROUPS):
+                    spread_bias(block, nc.vector.tensor_copy)
             for g in groups:
                 quantise_group(nc, grouped[g], g, packed["sat"])
             sum_squares_range(nc, junk, y_q, sumsq_q, first)
         q_rows = [rowpool.tile([P, D], BF16, tag="rows", name="q_rows%d" % b) for b in range(BATCH)]
-        inv_q = [inverse_norm(nc, small, sumsq_q, b, minus_half, "q%d" % b) for b in range(BATCH)]
+        inv_q = [inverse_norm(nc, small, sumsq_q[:, b, :], minus_half, "q%d" % b) for b in range(BATCH)]
         for g in range(GROUPS):
             for b in range(BATCH):
-                normalise_group(nc, y_q[b], inv_q[b], q_rows[b], g)
+                normalise(nc, y_q[b], inv_q[b], q_rows[b], g)
 
         y_k = [ypool.tile([P, D], F32, tag="y", name="y_k%d" % b) for b in range(BATCH)]
-        sumsq_k = small.tile([P, BATCH, D // BANK + 1], F32)
         bias_k = bias[:, D : 2 * D]
+        sums_k = [
+            small.tile([P, D // BANK], F32, name="sums_k0"),
+            small.tile([P, D // BANK + 1], F32, name="sums_k1"),
+        ]
+        chunks_of = {0: load_range(nc, wpool, Wk_words, 0)}
+
+        def multiply_pieces(pieces):
+            accs = [psum.tile([P, width], F32, tag="bank", name="piece") for b, start, width in pieces]
+            for g in range(GROUPS):
+                for acc, (b, start, width) in zip(accs, pieces):
+                    first = RANGE * (start // RANGE)
+                    multiply_pass(
+                        nc, acc, chunks_of[first][g], planes_k, packed["sat"], b, g, first, start, width
+                    )
+            return accs
+
+        done = [0, 0]
+
+        def add_bias_pieces(accs, pieces):
+            for acc, (b, start, width) in zip(accs, pieces):
+                add_bias(nc, acc, bias_k, y_k[b], start, width)
+
+        def sum_squares_pieces(pieces):
+            for b, start, width in pieces:
+                sum_squares(nc, junk, y_k[b], sums_k[b][:, done[b] : done[b] + 1], start, width)
+                done[b] += 1
+
+        pieces = [(b, BANK * h, BANK) for b in range(BATCH) for h in range(2)]
+        accs = multiply_pieces(pieces)
+        for first in (RANGE, 2 * RANGE):
+            chunks_of[first] = load_range(nc, wpool, Wk_words, first)
+        add_bias_pieces(accs, pieces)
         q_grouped = {}
-        for first in (0, RANGE):
-            acc = open_range(psum)
-            chunks = load_range(nc, wpool, Wk_words, first)
-            multiply_range(nc, acc, chunks, planes_k, packed["sat"], first)
-            add_bias_range(nc, acc, bias_k, y_k, first)
-            if first == RANGE:
-                for g in range(GROUPS):
-                    q_grouped[g] = flip_group(nc, psum, stage, identity, q_rows, half_of_the_words, g, nc.scalar.copy)
-            sum_squares_range(nc, junk, y_k, sumsq_k, first)
-        last_range = 2 * RANGE
-        chunks = load_range(nc, wpool, Wk_words, last_range)
-        k_rows = [rowpool.tile([P, D], BF16, tag="rows", name="k_rows%d" % b) for b in range(BATCH)]
-        pieces = [(last_range, BANK), (last_range + BANK, BANK // 2), (last_range + 3 * BANK // 2, BANK // 2)]
-        k_grouped = {}
-        inv_k = {}
-        for b in range(BATCH):
-            for i, (start, width) in enumerate(pieces):
-                piece = psum.tile([P, width], F32, tag="bank", name="piece")
-                for g in range(GROUPS):
-                    multiply_pass(nc, piece, chunks[g], planes_k, packed["sat"], b, g, last_range, start, width)
-                square_sum = sumsq_k[:, b, 4 + i : 5 + i]
-                add_bias(nc, piece, bias_k, y_k[b], start, width)
-                sum_squares(nc, junk, y_k[b], square_sum, start, width)
-                if b == 0 and i == 0:
-                    for g in range(GROUPS):
-                        quantise_group(nc, q_grouped[g], g, packed["q"])
-                if b == 1 and i == 0:
-                    for g in range(GROUPS):
-                        normalise_group(nc, y_k[0], inv_k[0], k_rows[0], g)
-            inv_k[b] = inverse_norm(nc, small, sumsq_k, b, minus_half, "k%d" % b)
         for g in range(GROUPS):
-            copy = nc.vector.tensor_copy if g < GROUPS // 2 else nc.scalar.copy
+            q_grouped[g] = flip_group(nc, psum, stage, identity, q_rows, half_of_the_words, g, nc.scalar.copy)
+        sum_squares_pieces(pieces)
+        pieces = [(0, 2 * BANK, BANK), (0, 3 * BANK, BANK), (1, 2 * BANK, BANK)]
+        accs = multiply_pieces(pieces)
+        for g in range(GROUPS):
+            quantise_group(nc, q_grouped[g], g, packed["q"])
+        add_bias_pieces(accs, pieces)
+        sum_squares_pieces(pieces)
+        pieces = [(0, 4 * BANK, BANK), (0, 5 * BANK, BANK)]
+        accs = multiply_pieces(pieces)
+        add_bias_pieces(accs, pieces)
+        sum_squares_pieces(pieces)
+        inv_k = inverse_norm(nc, small, sums_k[0], minus_half, "k0")
+        k_rows = [rowpool.tile([P, D], BF16, tag="rows", name="k_rows%d" % b) for b in range(BATCH)]
+        half = BANK // 2
+        for start, width in ((3 * BANK, BANK), (4 * BANK, BANK), (5 * BANK, half), (5 * BANK + half, half)):
+            pieces = [(1, start, width)]
+            accs = multiply_pieces(pieces)
+            add_bias_pieces(accs, pieces)
+            sum_squares_pieces(pieces)
+            if start == 3 * BANK:
+                normalise(nc, y_k[0], inv_k, k_rows[0], 4, on_scalar=True)
+                normalise(nc, y_k[0], inv_k, k_rows[0], 5, on_scalar=True)
+                for first in (0, 2):
+                    normalise(nc, y_k[0], inv_k, k_rows[0], first, count=2)
+        inv_k = inverse_norm(nc, small, sums_k[1], minus_half, "k1")
+        k_grouped = {}
+        for g in range(GROUPS):
+            copy = nc.vector.tensor_copy if g % 2 == 0 else nc.scalar.copy
             k_grouped[g] = flip_rows(nc, psum, stage, identity, k_rows[0], g, copy)
         for g in range(GROUPS):
             quantise_rows(nc, k_grouped[g], g, 0, packed["k"])
         sims = {0: multiply_sim(nc, psum, packed, 0)}
-        normalise_group(nc, y_k[1], inv_k[1], k_rows[1], GROUPS - 1, on_scalar=True)
+        normalise(nc, y_k[1], inv_k, k_rows[1], 5, on_scalar=True)
+        for first, count in ((0, 1), (1, 2), (3, 2)):
+            normalise(nc, y_k[1], inv_k, k_rows[1], first, count=count)
         for g in range(GROUPS):
-            if g < GROUPS - 1:
-                normalise_group(nc, y_k[1], inv_k[1], k_rows[1], g)
             k_grouped[g] = flip_rows(nc, psum, stage, identity, k_rows[1], g, nc.scalar.copy)
         for g in range(GROUPS):
             quantise_rows(nc, k_grouped[g], g, 1, packed["k"])
@@ -359,37 +395,40 @@ def tile_sinkhornot_w_kernel(
         for it in range(NUM_ITERS):
             if it > 0:
                 for b in range(BATCH):
+                    col_sum = psum.tile([P, 1], F32, tag="bank", name="col_sum%d" % b)
+                    nc.tensor.matmul(col_sum[:], lhsT=kern[b][:], rhs=u[b][:], start=True, stop=True)
+                    v[b] = turn.tile([P, 1], F32, name="v%d" % b)
+                    nc.vector.reciprocal(out=v[b][:], in_=col_sum[:])
+                for b in range(BATCH):
                     row_sum = psum.tile([P, 1], F32, tag="bank", name="row_sum%d" % b)
                     nc.tensor.matmul(row_sum[:], lhsT=kern_t[b][:], rhs=v[b][:], start=True, stop=True)
                     u[b] = turn.tile([P, 1], F32, name="u%d" % b)
                     nc.vector.reciprocal(out=u[b][:], in_=row_sum[:])
+
+        col_sum_all = [psum.tile([P, P], F32, tag="bank", name="col_sum_all%d" % b) for b in range(BATCH)]
+        w_all = [psum.tile([P, P], F32, tag="bank", name="w_all%d" % b) for b in range(BATCH)]
+        for rows, table in ((col_sum_all, kern), (w_all, kern_cost)):
             for b in range(BATCH):
-                col_sum = psum.tile([P, 1], F32, tag="bank", name="col_sum%d" % b)
-                nc.tensor.matmul(col_sum[:], lhsT=kern[b][:], rhs=u[b][:], start=True, stop=True)
-                v[b] = turn.tile([P, 1], F32, name="v%d" % b)
-                nc.vector.reciprocal(out=v[b][:], in_=col_sum[:])
-
-        w = [small.tile([P, 1], F32, name="w%d" % b) for b in range(BATCH)]
+                nc.tensor.matmul(
+                    rows[b][:], lhsT=u[b][:].to_broadcast([P, P]), rhs=table[b][:], start=True, stop=True
+                )
+        v_all = [small.tile([P, P], F32, name="v_all%d" % b) for b in range(BATCH)]
         for b in range(BATCH):
-            cost_sum = psum.tile([P, 1], F32, tag="bank", name="cost_sum%d" % b)
-            nc.tensor.matmul(cost_sum[:], lhsT=kern_cost[b][:], rhs=u[b][:], start=True, stop=True)
-            nc.scalar.copy(out=w[b][:], in_=cost_sum[:])
-
-        for b in range(BATCH):
-            v_all = psum.tile([P, P], F32, tag="bank", name="v_all%d" % b)
-            nc.tensor.matmul(v_all[:], lhsT=v[b][:].to_broadcast([P, P]), rhs=identity[:], start=True, stop=True)
+            nc.vector.reciprocal(out=v_all[b][:], in_=col_sum_all[b][:])
             plan = small.tile([P, P], F32, name="plan%d" % b)
             nc.vector.scalar_tensor_tensor(
-                out=plan[:], in0=kern[b][:], scalar=u[b][:], in1=v_all[:], op0=ALU.mult, op1=ALU.mult
+                out=plan[:], in0=kern[b][:], scalar=u[b][:], in1=v_all[b][:], op0=ALU.mult, op1=ALU.mult
             )
             nc.sync.dma_start(out=out_0[b], in_=plan[:])
-        ot_sum = psum.tile([P, 1], F32, tag="bank")
+        share = [small.tile([P, 1], F32, name="share%d" % b) for b in range(BATCH)]
         for b in range(BATCH):
-            nc.tensor.matmul(
-                ot_sum[:], lhsT=w[b][:].to_broadcast([P, P]), rhs=v[b][:], start=(b == 0), stop=(b == BATCH - 1)
+            products = small.tile([P, P], F32, name="products%d" % b)
+            nc.vector.scalar_tensor_tensor(
+                out=products[:], in0=v_all[b][:], scalar=1.0 / BATCH, in1=w_all[b][:], op0=ALU.mult, op1=ALU.mult,
+                accum_out=share[b][:],
             )
         ot_cost = small.tile([P, 1], F32)
-        nc.vector.tensor_scalar_mul(out=ot_cost[:], in0=ot_sum[:], scalar1=1.0 / BATCH)
+        nc.vector.tensor_tensor(out=ot_cost[:], in0=share[0][:], in1=share[1][:], op=ALU.add)
         ot_dst = out_1
         for missing in range(2 - out_1.ndim):
             ot_dst = ot_dst.unsqueeze(0)

@@ -23,7 +23,6 @@ BANK = 512
 RANGE = 2 * BANK
 PLANES_PER_SLOT = 4
 QUANT_LAG = 2
-WARM_UPS = 5
 NUM_ITERS = 5
 INV_REG = 10.0
 EPS = 1e-12
@@ -101,10 +100,8 @@ def multiply_pass(nc, acc, chunk, planes, x_packed, b, g, first, start, width):
     )
 
 
-def multiply_range(nc, acc, chunks, planes, x_packed, first, halfway=None):
+def multiply_range(nc, acc, chunks, planes, x_packed, first):
     for g in range(GROUPS):
-        if halfway and g == GROUPS // 2:
-            halfway()
         for b in range(BATCH):
             for h in range(2):
                 multiply_pass(nc, acc[b][h], chunks[g], planes, x_packed, b, g, first, first + BANK * h, BANK)
@@ -216,9 +213,11 @@ def tile_sinkhornot_w_kernel(
         bias_row = keep.tile([P, 2 * D], BF16)
         nc.vector.memset(bias_row[:, 0:D].bitcast(I32), 0)
         nc.vector.memset(planes_q[:].bitcast(I32), 0)
+        nc.vector.memset(bias_row[:, D : 2 * D].bitcast(I32), 0)
+        nc.vector.memset(planes_k[:].bitcast(I32), 0)
         identity = const.tile([P, P], F32)
         make_identity(nc, identity[:])
-        ones = const.tile([P, BANK], BF16)
+        ones = const.tile([P, P], BF16)
         nc.gpsimd.memset(ones[:], 1.0)
         minus_half = const.tile([P, 1], F32)
         nc.gpsimd.memset(minus_half[:], -0.5)
@@ -227,12 +226,16 @@ def tile_sinkhornot_w_kernel(
 
         drone = [rowpool.tile([P, D], BF16, tag="rows", name="drone%d" % b) for b in range(BATCH)]
         sat = [rowpool.tile([P, D], BF16, tag="rows", name="sat%d" % b) for b in range(BATCH)]
-        nc.scalar.activation(out=warm[:], in_=warm[:], func=ACT.Exp)
         nc.scalar.dma_start(out=bias_row[0:1, 0:D], in_=bq.unsqueeze(0))
+        nc.scalar.dma_start(out=bias_row[0:1, D : 2 * D], in_=bk.unsqueeze(0))
+        nc.scalar.activation(out=warm[:], in_=warm[:], func=ACT.Exp)
         for half in (slice(0, D // 2), slice(D // 2, D)):
             for b in range(BATCH):
                 nc.sync.dma_start(out=drone[b][:, half], in_=drone_tokens[b][:, half])
-        load_scale_planes(nc.sync.dma_start, planes_q, Wq_scales, I32)
+        for b in range(BATCH):
+            nc.sync.dma_start(out=sat[b][:], in_=sat_tokens[b])
+        load_scale_planes(nc.gpsimd.dma_start, planes_q, Wq_scales, F32)
+        load_scale_planes(nc.gpsimd.dma_start, planes_k, Wk_scales, F32)
 
         packed = {}
         for name in ("drone", "sat", "q", "k"):
@@ -241,53 +244,33 @@ def tile_sinkhornot_w_kernel(
                 keep.tile([P, GROUPS, BATCH * P], U8, align_bytes=64, name=name + "_scales"),
             )
         bias = keep.tile([P, 2 * D], BF16)
+        copies = (nc.scalar.copy, nc.vector.tensor_copy)
+        tokens_of = ((drone, packed["drone"]), (sat, packed["sat"]))
         grouped = {}
-
-        def spread_bias(block, copy):
-            cols = slice(BANK * block, BANK * (block + 1))
-            spread = psum.tile([P, BANK], BF16, tag="bank", name="spread")
-            nc.tensor.matmul(spread[:], lhsT=ones[:, 0:P], rhs=bias_row[:, cols], start=True, stop=True)
-            copy(out=bias[:, cols], in_=spread[:])
-
-        def spread_bq():
-            for block in range(GROUPS):
-                spread_bias(block, nc.scalar.copy)
-
-        for i in range(WARM_UPS):
-            dummy = psum.tile([P, BANK], F32, tag="bank", name="dummy")
-            nc.tensor.matmul(dummy[:], lhsT=ones[:, 0:P], rhs=ones[:], start=True, stop=True)
-        for s in range(GROUPS + QUANT_LAG):
-            if s < GROUPS:
-                copy = (nc.scalar.copy, nc.vector.tensor_copy)[s % 2]
-                grouped[s] = flip_group(nc, psum, stage, identity, drone, every_second_word, s, copy)
+        for s in range(2 * GROUPS + QUANT_LAG):
+            if s < 2 * GROUPS:
+                grouped[s] = flip_group(
+                    nc, psum, stage, identity, tokens_of[s // GROUPS][0], every_second_word, s % GROUPS, copies[s % 2]
+                )
+                if s % 2 == 0:
+                    spread = psum.tile([P, 2 * BANK], BF16, tag="bank")
+                nc.tensor.matmul(
+                    spread[:, BANK * (s % 2) : BANK * (s % 2 + 1)], lhsT=ones[:],
+                    rhs=bias_row[:, BANK * s : BANK * (s + 1)], start=True, stop=True,
+                )
+                if s % 2 == 1:
+                    nc.scalar.copy(out=bias[:, BANK * (s - 1) : BANK * (s + 1)], in_=spread[:])
             if s >= QUANT_LAG:
-                quantise_group(nc, grouped[s - QUANT_LAG], s - QUANT_LAG, packed["drone"])
-
-        nc.vector.memset(bias_row[:, D : 2 * D].bitcast(I32), 0)
-        nc.scalar.dma_start(out=bias_row[0:1, D : 2 * D], in_=bk.unsqueeze(0))
-        nc.vector.memset(planes_k[:].bitcast(I32), 0)
-        load_scale_planes(nc.gpsimd.dma_start, planes_k, Wk_scales, F32)
+                done = s - QUANT_LAG
+                quantise_group(nc, grouped[done], done % GROUPS, tokens_of[done // GROUPS][1])
 
         y_q = [ypool.tile([P, D], F32, tag="y", name="y_q%d" % b) for b in range(BATCH)]
         sumsq_q = small.tile([P, BATCH, D // BANK], F32)
         for first in range(0, D, RANGE):
             acc = open_range(psum)
             chunks = load_range(nc, wpool, Wq_words, first)
-            if first == 0:
-                for b in range(BATCH):
-                    nc.sync.dma_start(out=sat[b][:], in_=sat_tokens[b])
-            multiply_range(
-                nc, acc, chunks, planes_q, packed["drone"], first, halfway=spread_bq if first == 0 else None
-            )
+            multiply_range(nc, acc, chunks, planes_q, packed["drone"], first)
             add_bias_range(nc, acc, bias[:, 0:D], y_q, first)
-            groups = range(3 * (first // RANGE), 3 * (first // RANGE) + 3) if first < 2 * RANGE else ()
-            for g in groups:
-                grouped[g] = flip_group(nc, psum, stage, identity, sat, every_second_word, g, nc.scalar.copy)
-            if first == RANGE:
-                for block in range(GROUPS, 2 * GROUPS):
-                    spread_bias(block, nc.vector.tensor_copy)
-            for g in groups:
-                quantise_group(nc, grouped[g], g, packed["sat"])
             sum_squares_range(nc, junk, y_q, sumsq_q, first)
         q_rows = [rowpool.tile([P, D], BF16, tag="rows", name="q_rows%d" % b) for b in range(BATCH)]
         inv_q = [inverse_norm(nc, small, sumsq_q[:, b, :], minus_half, "q%d" % b) for b in range(BATCH)]

@@ -153,23 +153,24 @@ def normalise(nc, y, inv, rows, first, count=1, on_scalar=False):
         nc.vector.tensor_scalar_mul(out=rows[:, cols], in0=y[:, cols], scalar1=inv[:])
 
 
-def flip_rows(nc, psum, stage, identity, rows, g, copy):
+def flip_pair(nc, psum, stage, identity, rows, pair, copy):
     words = rows[:].bitcast(F32)
-    flipped = psum.tile([P, 2, P], F32, tag="bank", name="flipped_rows")
-    for u in range(2):
-        nc.tensor.transpose(flipped[:, u, :], words[:, half_of_the_words(g, u)], identity[:])
-    grouped = stage.tile([P, P, 2], F32, align_bytes=64, tag="grouped_rows", name="grouped_rows")
-    copy(out=grouped[:], in_=flipped[:].rearrange("p u r -> p r u"))
+    flipped = psum.tile([P, 2, 2, P], F32, tag="bank", name="flipped_pair")
+    for i in range(2):
+        for u in range(2):
+            nc.tensor.transpose(flipped[:, i, u, :], words[:, half_of_the_words(2 * pair + i, u)], identity[:])
+    grouped = stage.tile([P, 2, P, 2], F32, align_bytes=64, tag="grouped_pair", name="grouped_pair")
+    copy(out=grouped[:], in_=flipped[:].rearrange("p i u r -> p i r u"))
     return grouped
 
 
-def quantise_rows(nc, grouped, g, b, packed):
+def quantise_pair(nc, grouped, pair, packed):
     codes, scales = packed
-    tokens = slice(P * b, P * (b + 1))
+    both = slice(2 * pair, 2 * pair + 2)
     nc.vector.quantize_mx(
-        out=codes[:, g, tokens].bitcast(FP8X4),
-        scales=scales[:, g, tokens],
-        in_=grouped[:].rearrange("p r u -> p (r u)").bitcast(BF16),
+        out=codes[:, both, :].rearrange("p i r -> p (i r)").bitcast(FP8X4),
+        scales=scales[:, both, :].rearrange("p i r -> p (i r)"),
+        in_=grouped[:].rearrange("p i r u -> p (i r u)").bitcast(BF16),
     )
 
 
@@ -177,14 +178,18 @@ def multiply_sim(nc, psum, packed, b):
     sim = psum.tile([P, P], F32, tag="bank", name="sim%d" % b)
     sim_t = psum.tile([P, P], F32, tag="bank", name="sim_t%d" % b)
     tokens = slice(P * b, P * (b + 1))
+    q_codes, q_scales = packed["q"]
+    k_codes, k_scales = packed["k"][b]
     for g in range(GROUPS):
-        for out, left, right in ((sim, "q", "k"), (sim_t, "k", "q")):
+        q_side = (q_codes[:, g, tokens].bitcast(FP8X4), q_scales[:, g, tokens])
+        k_side = (k_codes[:, g, :].bitcast(FP8X4), k_scales[:, g, :])
+        for out, (lhs, lhs_scale), (rhs, rhs_scale) in ((sim, q_side, k_side), (sim_t, k_side, q_side)):
             nc.tensor.matmul_mx(
                 out=out[:],
-                lhsT=packed[left][0][:, g, tokens].bitcast(FP8X4),
-                lhsT_scale=packed[left][1][:, g, tokens],
-                rhs=packed[right][0][:, g, tokens].bitcast(FP8X4),
-                rhs_scale=packed[right][1][:, g, tokens],
+                lhsT=lhs,
+                lhsT_scale=lhs_scale,
+                rhs=rhs,
+                rhs_scale=rhs_scale,
                 start=(g == 0),
                 stop=(g == GROUPS - 1),
             )
@@ -202,7 +207,7 @@ def tile_sinkhornot_w_kernel(
         turn = ctx.enter_context(tc.tile_pool(name="turn", bufs=2))
         rowpool = ctx.enter_context(tc.tile_pool(name="rowpool", bufs=4))
         ypool = ctx.enter_context(tc.tile_pool(name="ypool", bufs=4))
-        wpool = ctx.enter_context(tc.tile_pool(name="wpool", bufs=16))
+        wpool = ctx.enter_context(tc.tile_pool(name="wpool", bufs=12))
         stage = ctx.enter_context(tc.tile_pool(name="stage", bufs=GROUPS))
         junk = ctx.enter_context(tc.tile_pool(name="junk", bufs=2))
         psum = ctx.enter_context(tc.psum_pool(name="psum", bufs=8))
@@ -238,15 +243,28 @@ def tile_sinkhornot_w_kernel(
         load_scale_planes(nc.gpsimd.dma_start, planes_k, Wk_scales, F32)
 
         packed = {}
-        for name in ("drone", "sat", "q", "k"):
+        for name in ("drone", "sat", "q"):
             packed[name] = (
                 keep.tile([P, GROUPS, BATCH * P], U32, align_bytes=64, name=name + "_codes"),
                 keep.tile([P, GROUPS, BATCH * P], U8, align_bytes=64, name=name + "_scales"),
             )
+        packed["k"] = [
+            (
+                keep.tile([P, GROUPS, P], U32, align_bytes=64, name="k_codes%d" % b),
+                keep.tile([P, GROUPS, P], U8, align_bytes=64, name="k_scales%d" % b),
+            )
+            for b in range(BATCH)
+        ]
         bias = keep.tile([P, 2 * D], BF16)
         copies = (nc.scalar.copy, nc.vector.tensor_copy)
         tokens_of = ((drone, packed["drone"]), (sat, packed["sat"]))
         grouped = {}
+
+        def keep_clock(count):
+            for i in range(count):
+                dummy = psum.tile([P, BANK], F32, tag="bank", name="dummy")
+                nc.tensor.matmul(dummy[:], lhsT=ones[:], rhs=bias_row[:, 0:BANK], start=True, stop=True)
+
         for s in range(2 * GROUPS + QUANT_LAG):
             if s < 2 * GROUPS:
                 grouped[s] = flip_group(
@@ -328,32 +346,50 @@ def tile_sinkhornot_w_kernel(
         sum_squares_pieces(pieces)
         inv_k = inverse_norm(nc, small, sums_k[0], minus_half, "k0")
         k_rows = [rowpool.tile([P, D], BF16, tag="rows", name="k_rows%d" % b) for b in range(BATCH)]
-        half = BANK // 2
-        for start, width in ((3 * BANK, BANK), (4 * BANK, BANK), (5 * BANK, half), (5 * BANK + half, half)):
+        last_pieces = [(3 * BANK, BANK), (4 * BANK, BANK), (5 * BANK, BANK // 2), (D - BANK // 2, BANK // 4)]
+        for start, width in last_pieces:
             pieces = [(1, start, width)]
             accs = multiply_pieces(pieces)
             add_bias_pieces(accs, pieces)
             sum_squares_pieces(pieces)
-            if start == 3 * BANK:
-                normalise(nc, y_k[0], inv_k, k_rows[0], 4, on_scalar=True)
-                normalise(nc, y_k[0], inv_k, k_rows[0], 5, on_scalar=True)
-                for first in (0, 2):
-                    normalise(nc, y_k[0], inv_k, k_rows[0], first, count=2)
-        inv_k = inverse_norm(nc, small, sums_k[1], minus_half, "k1")
+            if start == 5 * BANK:
+                normalise(nc, y_k[0], inv_k, k_rows[0], 0, count=2)
+        pieces = [(1, D - BANK // 4, BANK // 4)]
+        accs = multiply_pieces(pieces)
+        add_bias_pieces(accs, pieces)
+        last_y = y_k[1][:, D - BANK // 4 : D]
+        squares = junk.tile([P, BANK // 4], F32)
+        last_sum = small.tile([P, 1], F32)
+        nc.vector.scalar_tensor_tensor(
+            out=squares[:], in0=last_y, scalar=1.0, in1=last_y, op0=ALU.mult, op1=ALU.mult, accum_out=last_sum[:]
+        )
+        first_sums = small.tile([P, 1], F32)
+        nc.vector.tensor_reduce(out=first_sums[:], in_=sums_k[1][:, 0 : done[1]], axis=AXIS.X, op=ALU.add)
+        total = small.tile([P, 1], F32)
+        nc.vector.tensor_scalar(
+            out=total[:], in0=last_sum[:], scalar1=first_sums[:], scalar2=EPS * EPS, op0=ALU.add, op1=ALU.max
+        )
+        inv_k1 = small.tile([P, 1], F32)
+        nc.gpsimd.tensor_tensor(out=inv_k1[:], in0=total[:], in1=minus_half[:], op=ALU.pow)
+
+        pairs = range(GROUPS // 2)
         k_grouped = {}
-        for g in range(GROUPS):
-            copy = nc.vector.tensor_copy if g % 2 == 0 else nc.scalar.copy
-            k_grouped[g] = flip_rows(nc, psum, stage, identity, k_rows[0], g, copy)
-        for g in range(GROUPS):
-            quantise_rows(nc, k_grouped[g], g, 0, packed["k"])
+        for pair in (1, 2):
+            normalise(nc, y_k[0], inv_k, k_rows[0], 2 * pair, count=2)
+        for pair in pairs:
+            k_grouped[0, pair] = flip_pair(nc, psum, stage, identity, k_rows[0], pair, nc.scalar.copy)
+        keep_clock(2)
+        for pair in pairs:
+            normalise(nc, y_k[1], inv_k1, k_rows[1], 2 * pair, count=2)
+        for pair in pairs:
+            quantise_pair(nc, k_grouped[0, pair], pair, packed["k"][0])
+        for pair in pairs:
+            k_grouped[1, pair] = flip_pair(nc, psum, stage, identity, k_rows[1], pair, nc.scalar.copy)
+        keep_clock(1)
         sims = {0: multiply_sim(nc, psum, packed, 0)}
-        normalise(nc, y_k[1], inv_k, k_rows[1], 5, on_scalar=True)
-        for first, count in ((0, 1), (1, 2), (3, 2)):
-            normalise(nc, y_k[1], inv_k, k_rows[1], first, count=count)
-        for g in range(GROUPS):
-            k_grouped[g] = flip_rows(nc, psum, stage, identity, k_rows[1], g, nc.scalar.copy)
-        for g in range(GROUPS):
-            quantise_rows(nc, k_grouped[g], g, 1, packed["k"])
+        keep_clock(1)
+        for pair in pairs:
+            quantise_pair(nc, k_grouped[1, pair], pair, packed["k"][1])
 
         kern = [small.tile([P, P], F32, name="kern%d" % b) for b in range(BATCH)]
         kern_t = [small.tile([P, P], F32, name="kern_t%d" % b) for b in range(BATCH)]
@@ -382,36 +418,40 @@ def tile_sinkhornot_w_kernel(
                     nc.tensor.matmul(col_sum[:], lhsT=kern[b][:], rhs=u[b][:], start=True, stop=True)
                     v[b] = turn.tile([P, 1], F32, name="v%d" % b)
                     nc.vector.reciprocal(out=v[b][:], in_=col_sum[:])
+                keep_clock(1)
                 for b in range(BATCH):
                     row_sum = psum.tile([P, 1], F32, tag="bank", name="row_sum%d" % b)
                     nc.tensor.matmul(row_sum[:], lhsT=kern_t[b][:], rhs=v[b][:], start=True, stop=True)
                     u[b] = turn.tile([P, 1], F32, name="u%d" % b)
                     nc.vector.reciprocal(out=u[b][:], in_=row_sum[:])
+                keep_clock(1)
 
-        col_sum_all = [psum.tile([P, P], F32, tag="bank", name="col_sum_all%d" % b) for b in range(BATCH)]
-        w_all = [psum.tile([P, P], F32, tag="bank", name="w_all%d" % b) for b in range(BATCH)]
-        for rows, table in ((col_sum_all, kern), (w_all, kern_cost)):
-            for b in range(BATCH):
-                nc.tensor.matmul(
-                    rows[b][:], lhsT=u[b][:].to_broadcast([P, P]), rhs=table[b][:], start=True, stop=True
-                )
-        v_all = [small.tile([P, P], F32, name="v_all%d" % b) for b in range(BATCH)]
+        kern_u = [small.tile([P, P], F32, name="kern_u%d" % b) for b in range(BATCH)]
+        w = [small.tile([P, 1], F32, name="w%d" % b) for b in range(BATCH)]
         for b in range(BATCH):
-            nc.vector.reciprocal(out=v_all[b][:], in_=col_sum_all[b][:])
+            nc.scalar.activation(out=kern_u[b][:], in_=kern[b][:], func=ACT.Copy, scale=u[b][:])
+            col_sum = psum.tile([P, 1], F32, tag="bank", name="col_sum%d" % b)
+            nc.tensor.matmul(col_sum[:], lhsT=kern[b][:], rhs=u[b][:], start=True, stop=True)
+            v[b] = turn.tile([P, 1], F32, name="v%d" % b)
+            nc.vector.reciprocal(out=v[b][:], in_=col_sum[:])
+        for b in range(BATCH):
+            cost_sum = psum.tile([P, 1], F32, tag="bank", name="cost_sum%d" % b)
+            nc.tensor.matmul(cost_sum[:], lhsT=kern_cost[b][:], rhs=u[b][:], start=True, stop=True)
+            nc.scalar.copy(out=w[b][:], in_=cost_sum[:])
+
+        for b in range(BATCH):
+            v_all = psum.tile([P, P], F32, tag="bank", name="v_all%d" % b)
+            nc.tensor.matmul(v_all[:], lhsT=v[b][:].to_broadcast([P, P]), rhs=identity[:], start=True, stop=True)
             plan = small.tile([P, P], F32, name="plan%d" % b)
-            nc.vector.scalar_tensor_tensor(
-                out=plan[:], in0=kern[b][:], scalar=u[b][:], in1=v_all[b][:], op0=ALU.mult, op1=ALU.mult
-            )
+            nc.vector.tensor_tensor(out=plan[:], in0=kern_u[b][:], in1=v_all[:], op=ALU.mult)
             nc.sync.dma_start(out=out_0[b], in_=plan[:])
-        share = [small.tile([P, 1], F32, name="share%d" % b) for b in range(BATCH)]
+        ot_sum = psum.tile([P, 1], F32, tag="bank")
         for b in range(BATCH):
-            products = small.tile([P, P], F32, name="products%d" % b)
-            nc.vector.scalar_tensor_tensor(
-                out=products[:], in0=v_all[b][:], scalar=1.0 / BATCH, in1=w_all[b][:], op0=ALU.mult, op1=ALU.mult,
-                accum_out=share[b][:],
+            nc.tensor.matmul(
+                ot_sum[:], lhsT=w[b][:].to_broadcast([P, P]), rhs=v[b][:], start=(b == 0), stop=(b == BATCH - 1)
             )
         ot_cost = small.tile([P, 1], F32)
-        nc.vector.tensor_tensor(out=ot_cost[:], in0=share[0][:], in1=share[1][:], op=ALU.add)
+        nc.scalar.activation(out=ot_cost[:], in_=ot_sum[:], func=ACT.Copy, scale=1.0 / BATCH)
         ot_dst = out_1
         for missing in range(2 - out_1.ndim):
             ot_dst = ot_dst.unsqueeze(0)

from contextlib import ExitStack

import concourse.mybir as mybir
from concourse.masks import make_identity

F32 = mybir.dt.float32
BF16 = mybir.dt.bfloat16
I32 = mybir.dt.int32
U32 = mybir.dt.uint32
U8 = mybir.dt.uint8
FP8X4 = mybir.dt.float8_e4m3fn_x4
ALU = mybir.AluOpType
ACT = mybir.ActivationFunctionType
AXIS = mybir.AxisListType

P = 128
BATCH = 2
D = 3072
K_PASS = 512
GROUPS = D // K_PASS
WORDS = K_PASS // 2
BANK = 512
RANGE = 2 * BANK
PLANES_PER_SLOT = 4
QUANT_LAG = 2
NUM_ITERS = 5
INV_REG = 10.0
EPS = 1e-12

FLOPS = 2 * (2 * BATCH * P * D * D) + 2 * BATCH * P * P * D


def load_scale_planes(load, planes, scales, dtype):
    words = scales.bitcast(dtype)
    for first in range(0, GROUPS, PLANES_PER_SLOT):
        count = min(PLANES_PER_SLOT, GROUPS - first)
        for quadrant in range(4):
            load(
                out=planes[32 * quadrant : 32 * quadrant + 4 * count, first // PLANES_PER_SLOT, :].bitcast(dtype),
                in_=words[first : first + count, 4 * quadrant : 4 * quadrant + 4, :],
            )


def scale_plane(planes, g, cols):
    return planes[4 * (g % PLANES_PER_SLOT) : P, g // PLANES_PER_SLOT, cols]


def every_second_word(g, u):
    return slice(WORDS * g + u, WORDS * (g + 1), 2)


def half_of_the_words(g, u):
    return slice(WORDS * g + P * u, WORDS * g + P * (u + 1))


def flip_group(nc, psum, stage, identity, rows, word_cols, g, copy):
    flipped = psum.tile([P, BATCH, 2, P], F32, tag="bank")
    for b in range(BATCH):
        words = rows[b][:].bitcast(F32)
        for u in range(2):
            nc.tensor.transpose(flipped[:, b, u, :], words[:, word_cols(g, u)], identity[:])
    grouped = stage.tile([P, BATCH, P, 2], F32, align_bytes=64)
    copy(out=grouped[:], in_=flipped[:].rearrange("p b u r -> p b r u"))
    return grouped


def quantise_group(nc, grouped, g, packed):
    codes, scales = packed
    nc.vector.quantize_mx(
        out=codes[:, g, :].bitcast(FP8X4),
        scales=scales[:, g, :],
        in_=grouped[:].rearrange("p b r u -> p (b r u)").bitcast(BF16),
    )


def open_range(psum):
    return [[psum.tile([P, BANK], F32, tag="bank", name="acc%d%d" % (b, h)) for h in range(2)] for b in range(BATCH)]


def load_range(nc, wpool, w_words, first):
    words = w_words.rearrange("g p n t -> g p (n t)").bitcast(I32)
    chunks = []
    for g in range(GROUPS):
        chunk = wpool.tile([P, RANGE], U32, align_bytes=64, tag="chunk", name="chunk%d" % g)
        nc.sync.dma_start(out=chunk[:].bitcast(I32), in_=words[g, :, first : first + RANGE])
        chunks.append(chunk)
    return chunks


def multiply_pass(nc, acc, chunk, planes, x_packed, b, g, first, start, width):
    x_codes, x_scales = x_packed
    nc.tensor.matmul_mx(
        out=acc[:],
        lhsT=x_codes[:, g, P * b : P * (b + 1)].bitcast(FP8X4),
        lhsT_scale=x_scales[:, g, P * b : P * (b + 1)],
        rhs=chunk[:, start - first : start - first + width].bitcast(FP8X4),
        rhs_scale=scale_plane(planes, g, slice(start, start + width)),
        start=(g == 0),
        stop=(g == GROUPS - 1),
    )


def multiply_range(nc, acc, chunks, planes, x_packed, first):
    for g in range(GROUPS):
        for b in range(BATCH):
            for h in range(2):
                multiply_pass(nc, acc[b][h], chunks[g], planes, x_packed, b, g, first, first + BANK * h, BANK)


def add_bias(nc, acc, bias, y, start, width):
    cols = slice(start, start + width)
    nc.vector.tensor_tensor(out=y[:, cols], in0=acc[:], in1=bias[:, cols], op=ALU.add)


def sum_squares(nc, junk, y, square_sum, start, width):
    squares = junk.tile([P, BANK], BF16)
    nc.scalar.activation(
        out=squares[:, 0:width], in_=y[:, start : start + width], func=ACT.Square, accum_out=square_sum
    )


def add_bias_range(nc, acc, bias, y, first):
    for b in range(BATCH):
        for h in range(2):
            add_bias(nc, acc[b][h], bias, y[b], first + BANK * h, BANK)


def sum_squares_range(nc, junk, y, sumsq, first):
    for b in range(BATCH):
        for h in range(2):
            block = first // BANK + h
            sum_squares(nc, junk, y[b], sumsq[:, b, block : block + 1], first + BANK * h, BANK)


def inverse_norm(nc, small, sums, minus_half, name):
    last = sums.shape[1] - 1
    partial = small.tile([P, 1], F32, name=name + "_partial")
    nc.vector.tensor_reduce(out=partial[:], in_=sums[:, 0:last], axis=AXIS.X, op=ALU.add)
    total = small.tile([P, 1], F32, name=name + "_total")
    nc.gpsimd.tensor_scalar(
        out=total[:], in0=sums[:, last : last + 1], scalar1=partial[:], scalar2=EPS * EPS, op0=ALU.add, op1=ALU.max
    )
    inv = small.tile([P, 1], F32, name=name + "_inv")
    nc.gpsimd.tensor_tensor(out=inv[:], in0=total[:], in1=minus_half[:], op=ALU.pow)
    return inv


def normalise(nc, y, inv, rows, first, count=1, on_scalar=False):
    cols = slice(K_PASS * first, K_PASS * (first + count))
    if on_scalar:
        nc.scalar.activation(out=rows[:, cols], in_=y[:, cols], func=ACT.Copy, scale=inv[:])
    else:
        nc.vector.tensor_scalar_mul(out=rows[:, cols], in0=y[:, cols], scalar1=inv[:])


def flip_pair(nc, psum, stage, identity, rows, pair, copy):
    words = rows[:].bitcast(F32)
    flipped = psum.tile([P, 2, 2, P], F32, tag="bank", name="flipped_pair")
    for i in range(2):
        for u in range(2):
            nc.tensor.transpose(flipped[:, i, u, :], words[:, half_of_the_words(2 * pair + i, u)], identity[:])
    grouped = stage.tile([P, 2, P, 2], F32, align_bytes=64, tag="grouped_pair", name="grouped_pair")
    copy(out=grouped[:], in_=flipped[:].rearrange("p i u r -> p i r u"))
    return grouped


def quantise_pair(nc, grouped, pair, packed):
    codes, scales = packed
    both = slice(2 * pair, 2 * pair + 2)
    nc.vector.quantize_mx(
        out=codes[:, both, :].rearrange("p i r -> p (i r)").bitcast(FP8X4),
        scales=scales[:, both, :].rearrange("p i r -> p (i r)"),
        in_=grouped[:].rearrange("p i r u -> p (i r u)").bitcast(BF16),
    )


def multiply_sim(nc, psum, packed, b):
    sim = psum.tile([P, P], F32, tag="bank", name="sim%d" % b)
    sim_t = psum.tile([P, P], F32, tag="bank", name="sim_t%d" % b)
    tokens = slice(P * b, P * (b + 1))
    q_codes, q_scales = packed["q"]
    k_codes, k_scales = packed["k"][b]
    for g in range(GROUPS):
        q_side = (q_codes[:, g, tokens].bitcast(FP8X4), q_scales[:, g, tokens])
        k_side = (k_codes[:, g, :].bitcast(FP8X4), k_scales[:, g, :])
        for out, (lhs, lhs_scale), (rhs, rhs_scale) in ((sim, q_side, k_side), (sim_t, k_side, q_side)):
            nc.tensor.matmul_mx(
                out=out[:],
                lhsT=lhs,
                lhsT_scale=lhs_scale,
                rhs=rhs,
                rhs_scale=rhs_scale,
                start=(g == 0),
                stop=(g == GROUPS - 1),
            )
    return sim, sim_t


def tile_sinkhornot_w_kernel(
    tc, drone_tokens, sat_tokens, Wq_words, Wq_scales, bq, Wk_words, Wk_scales, bk, out_0, out_1
):
    nc = tc.nc
    with ExitStack() as ctx:
        const = ctx.enter_context(tc.tile_pool(name="const", bufs=1))
        keep = ctx.enter_context(tc.tile_pool(name="keep", bufs=1))
        small = ctx.enter_context(tc.tile_pool(name="small", bufs=1))
        turn = ctx.enter_context(tc.tile_pool(name="turn", bufs=2))
        rowpool = ctx.enter_context(tc.tile_pool(name="rowpool", bufs=4))
        ypool = ctx.enter_context(tc.tile_pool(name="ypool", bufs=4))
        wpool = ctx.enter_context(tc.tile_pool(name="wpool", bufs=12))
        stage = ctx.enter_context(tc.tile_pool(name="stage", bufs=GROUPS))
        junk = ctx.enter_context(tc.tile_pool(name="junk", bufs=2))
        psum = ctx.enter_context(tc.psum_pool(name="psum", bufs=8))
        ctx.enter_context(tc.manual_schedule())

        planes_q = keep.tile([P, 2, D], U8, align_bytes=64)
        planes_k = keep.tile([P, 2, D], U8, align_bytes=64)
        bias_row = keep.tile([P, 2 * D], BF16)
        nc.vector.memset(bias_row[:, 0:D].bitcast(I32), 0)
        nc.vector.memset(planes_q[:].bitcast(I32), 0)
        nc.vector.memset(bias_row[:, D : 2 * D].bitcast(I32), 0)
        nc.vector.memset(planes_k[:].bitcast(I32), 0)
        identity = const.tile([P, P], F32)
        make_identity(nc, identity[:])
        ones = const.tile([P, P], BF16)
        nc.gpsimd.memset(ones[:], 1.0)
        minus_half = const.tile([P, 1], F32)
        nc.gpsimd.memset(minus_half[:], -0.5)
        warm = const.tile([P, 1], F32)
        nc.gpsimd.memset(warm[:], 0.0)

        drone = [rowpool.tile([P, D], BF16, tag="rows", name="drone%d" % b) for b in range(BATCH)]
        sat = [rowpool.tile([P, D], BF16, tag="rows", name="sat%d" % b) for b in range(BATCH)]
        nc.scalar.dma_start(out=bias_row[0:1, 0:D], in_=bq.unsqueeze(0))
        nc.scalar.dma_start(out=bias_row[0:1, D : 2 * D], in_=bk.unsqueeze(0))
        nc.scalar.activation(out=warm[:], in_=warm[:], func=ACT.Exp)
        for half in (slice(0, D // 2), slice(D // 2, D)):
            for b in range(BATCH):
                nc.sync.dma_start(out=drone[b][:, half], in_=drone_tokens[b][:, half])
        for b in range(BATCH):
            nc.sync.dma_start(out=sat[b][:], in_=sat_tokens[b])
        load_scale_planes(nc.gpsimd.dma_start, planes_q, Wq_scales, F32)
        load_scale_planes(nc.gpsimd.dma_start, planes_k, Wk_scales, F32)

        packed = {}
        for name in ("drone", "sat", "q"):
            packed[name] = (
                keep.tile([P, GROUPS, BATCH * P], U32, align_bytes=64, name=name + "_codes"),
                keep.tile([P, GROUPS, BATCH * P], U8, align_bytes=64, name=name + "_scales"),
            )
        packed["k"] = [
            (
                keep.tile([P, GROUPS, P], U32, align_bytes=64, name="k_codes%d" % b),
                keep.tile([P, GROUPS, P], U8, align_bytes=64, name="k_scales%d" % b),
            )
            for b in range(BATCH)
        ]
        bias = keep.tile([P, 2 * D], BF16)
        copies = (nc.scalar.copy, nc.vector.tensor_copy)
        tokens_of = ((drone, packed["drone"]), (sat, packed["sat"]))
        grouped = {}

        def keep_clock(count):
            for i in range(count):
                dummy = psum.tile([P, BANK], F32, tag="bank", name="dummy")
                nc.tensor.matmul(dummy[:], lhsT=ones[:], rhs=bias_row[:, 0:BANK], start=True, stop=True)

        for s in range(2 * GROUPS + QUANT_LAG):
            if s < 2 * GROUPS:
                grouped[s] = flip_group(
                    nc, psum, stage, identity, tokens_of[s // GROUPS][0], every_second_word, s % GROUPS, copies[s % 2]
                )
                if s % 2 == 0:
                    spread = psum.tile([P, 2 * BANK], BF16, tag="bank")
                nc.tensor.matmul(
                    spread[:, BANK * (s % 2) : BANK * (s % 2 + 1)], lhsT=ones[:],
                    rhs=bias_row[:, BANK * s : BANK * (s + 1)], start=True, stop=True,
                )
                if s % 2 == 1:
                    nc.scalar.copy(out=bias[:, BANK * (s - 1) : BANK * (s + 1)], in_=spread[:])
            if s >= QUANT_LAG:
                done = s - QUANT_LAG
                quantise_group(nc, grouped[done], done % GROUPS, tokens_of[done // GROUPS][1])

        y_q = [ypool.tile([P, D], F32, tag="y", name="y_q%d" % b) for b in range(BATCH)]
        sumsq_q = small.tile([P, BATCH, D // BANK], F32)
        for first in range(0, D, RANGE):
            acc = open_range(psum)
            chunks = load_range(nc, wpool, Wq_words, first)
            multiply_range(nc, acc, chunks, planes_q, packed["drone"], first)
            add_bias_range(nc, acc, bias[:, 0:D], y_q, first)
            sum_squares_range(nc, junk, y_q, sumsq_q, first)
        q_rows = [rowpool.tile([P, D], BF16, tag="rows", name="q_rows%d" % b) for b in range(BATCH)]
        inv_q = [inverse_norm(nc, small, sumsq_q[:, b, :], minus_half, "q%d" % b) for b in range(BATCH)]
        for g in range(GROUPS):
            for b in range(BATCH):
                normalise(nc, y_q[b], inv_q[b], q_rows[b], g)

        y_k = [ypool.tile([P, D], F32, tag="y", name="y_k%d" % b) for b in range(BATCH)]
        bias_k = bias[:, D : 2 * D]
        sums_k = [
            small.tile([P, D // BANK], F32, name="sums_k0"),
            small.tile([P, D // BANK + 1], F32, name="sums_k1"),
        ]
        chunks_of = {0: load_range(nc, wpool, Wk_words, 0)}

        def multiply_pieces(pieces):
            accs = [psum.tile([P, width], F32, tag="bank", name="piece") for b, start, width in pieces]
            for g in range(GROUPS):
                for acc, (b, start, width) in zip(accs, pieces):
                    first = RANGE * (start // RANGE)
                    multiply_pass(
                        nc, acc, chunks_of[first][g], planes_k, packed["sat"], b, g, first, start, width
                    )
            return accs

        done = [0, 0]

        def add_bias_pieces(accs, pieces):
            for acc, (b, start, width) in zip(accs, pieces):
                add_bias(nc, acc, bias_k, y_k[b], start, width)

        def sum_squares_pieces(pieces):
            for b, start, width in pieces:
                sum_squares(nc, junk, y_k[b], sums_k[b][:, done[b] : done[b] + 1], start, width)
                done[b] += 1

        pieces = [(b, BANK * h, BANK) for b in range(BATCH) for h in range(2)]
        accs = multiply_pieces(pieces)
        for first in (RANGE, 2 * RANGE):
            chunks_of[first] = load_range(nc, wpool, Wk_words, first)
        add_bias_pieces(accs, pieces)
        q_grouped = {}
        for g in range(GROUPS):
            q_grouped[g] = flip_group(nc, psum, stage, identity, q_rows, half_of_the_words, g, nc.scalar.copy)
        sum_squares_pieces(pieces)
        pieces = [(0, 2 * BANK, BANK), (0, 3 * BANK, BANK), (1, 2 * BANK, BANK)]
        accs = multiply_pieces(pieces)
        for g in range(GROUPS):
            quantise_group(nc, q_grouped[g], g, packed["q"])
        add_bias_pieces(accs, pieces)
        sum_squares_pieces(pieces)
        pieces = [(0, 4 * BANK, BANK), (0, 5 * BANK, BANK)]
        accs = multiply_pieces(pieces)
        add_bias_pieces(accs, pieces)
        sum_squares_pieces(pieces)
        inv_k = inverse_norm(nc, small, sums_k[0], minus_half, "k0")
        k_rows = [rowpool.tile([P, D], BF16, tag="rows", name="k_rows%d" % b) for b in range(BATCH)]
        last_pieces = [(3 * BANK, BANK), (4 * BANK, BANK), (5 * BANK, BANK // 2), (D - BANK // 2, BANK // 4)]
        for start, width in last_pieces:
            pieces = [(1, start, width)]
            accs = multiply_pieces(pieces)
            add_bias_pieces(accs, pieces)
            sum_squares_pieces(pieces)
            if start == 5 * BANK:
                normalise(nc, y_k[0], inv_k, k_rows[0], 0, count=2)
        pieces = [(1, D - BANK // 4, BANK // 4)]
        accs = multiply_pieces(pieces)
        add_bias_pieces(accs, pieces)
        last_y = y_k[1][:, D - BANK // 4 : D]
        squares = junk.tile([P, BANK // 4], F32)
        last_sum = small.tile([P, 1], F32)
        nc.vector.scalar_tensor_tensor(
            out=squares[:], in0=last_y, scalar=1.0, in1=last_y, op0=ALU.mult, op1=ALU.mult, accum_out=last_sum[:]
        )
        first_sums = small.tile([P, 1], F32)
        nc.vector.tensor_reduce(out=first_sums[:], in_=sums_k[1][:, 0 : done[1]], axis=AXIS.X, op=ALU.add)
        total = small.tile([P, 1], F32)
        nc.vector.tensor_scalar(
            out=total[:], in0=last_sum[:], scalar1=first_sums[:], scalar2=EPS * EPS, op0=ALU.add, op1=ALU.max
        )
        inv_k1 = small.tile([P, 1], F32)
        nc.gpsimd.tensor_tensor(out=inv_k1[:], in0=total[:], in1=minus_half[:], op=ALU.pow)

        pairs = range(GROUPS // 2)
        k_grouped = {}
        for pair in (1, 2):
            normalise(nc, y_k[0], inv_k, k_rows[0], 2 * pair, count=2)
        for pair in pairs:
            k_grouped[0, pair] = flip_pair(nc, psum, stage, identity, k_rows[0], pair, nc.scalar.copy)
        keep_clock(2)
        for pair in pairs:
            normalise(nc, y_k[1], inv_k1, k_rows[1], 2 * pair, count=2)
        for pair in pairs:
            quantise_pair(nc, k_grouped[0, pair], pair, packed["k"][0])
        for pair in pairs:
            k_grouped[1, pair] = flip_pair(nc, psum, stage, identity, k_rows[1], pair, nc.scalar.copy)
        keep_clock(1)
        sims = {0: multiply_sim(nc, psum, packed, 0)}
        keep_clock(1)
        for pair in pairs:
            quantise_pair(nc, k_grouped[1, pair], pair, packed["k"][1])

        kern = [small.tile([P, P], F32, name="kern%d" % b) for b in range(BATCH)]
        kern_t = [small.tile([P, P], F32, name="kern_t%d" % b) for b in range(BATCH)]
        cost = [small.tile([P, P], F32, name="cost%d" % b) for b in range(BATCH)]
        kern_cost = [small.tile([P, P], F32, name="kern_cost%d" % b) for b in range(BATCH)]
        u = [None, None]
        v = [None, None]
        for b in range(BATCH):
            if b == 1:
                sims[1] = multiply_sim(nc, psum, packed, 1)
            sim, sim_t = sims[b]
            row_sum = turn.tile([P, 1], F32, name="first_row_sum%d" % b)
            nc.scalar.activation(
                out=kern[b][:], in_=sim[:], func=ACT.Exp, scale=INV_REG, bias=-INV_REG, accum_out=row_sum[:]
            )
            u[b] = turn.tile([P, 1], F32, name="u%d" % b)
            nc.vector.reciprocal(out=u[b][:], in_=row_sum[:])
            nc.scalar.activation(out=kern_t[b][:], in_=sim_t[:], func=ACT.Exp, scale=INV_REG, bias=-INV_REG)
            nc.scalar.activation(out=cost[b][:], in_=sim[:], func=ACT.Copy, scale=-1.0, bias=1.0)
            nc.gpsimd.tensor_tensor(out=kern_cost[b][:], in0=kern[b][:], in1=cost[b][:], op=ALU.mult)

        for it in range(NUM_ITERS):
            if it > 0:
                for b in range(BATCH):
                    col_sum = psum.tile([P, 1], F32, tag="bank", name="col_sum%d" % b)
                    nc.tensor.matmul(col_sum[:], lhsT=kern[b][:], rhs=u[b][:], start=True, stop=True)
                    v[b] = turn.tile([P, 1], F32, name="v%d" % b)
                    nc.vector.reciprocal(out=v[b][:], in_=col_sum[:])
                keep_clock(1)
                for b in range(BATCH):
                    row_sum = psum.tile([P, 1], F32, tag="bank", name="row_sum%d" % b)
                    nc.tensor.matmul(row_sum[:], lhsT=kern_t[b][:], rhs=v[b][:], start=True, stop=True)
                    u[b] = turn.tile([P, 1], F32, name="u%d" % b)
                    nc.vector.reciprocal(out=u[b][:], in_=row_sum[:])
                keep_clock(1)

        kern_u = [small.tile([P, P], F32, name="kern_u%d" % b) for b in range(BATCH)]
        w = [small.tile([P, 1], F32, name="w%d" % b) for b in range(BATCH)]
        for b in range(BATCH):
            nc.scalar.activation(out=kern_u[b][:], in_=kern[b][:], func=ACT.Copy, scale=u[b][:])
            col_sum = psum.tile([P, 1], F32, tag="bank", name="col_sum%d" % b)
            nc.tensor.matmul(col_sum[:], lhsT=kern[b][:], rhs=u[b][:], start=True, stop=True)
            v[b] = turn.tile([P, 1], F32, name="v%d" % b)
            nc.vector.reciprocal(out=v[b][:], in_=col_sum[:])
        for b in range(BATCH):
            cost_sum = psum.tile([P, 1], F32, tag="bank", name="cost_sum%d" % b)
            nc.tensor.matmul(cost_sum[:], lhsT=kern_cost[b][:], rhs=u[b][:], start=True, stop=True)
            nc.scalar.copy(out=w[b][:], in_=cost_sum[:])

        for b in range(BATCH):
            v_all = psum.tile([P, P], F32, tag="bank", name="v_all%d" % b)
            nc.tensor.matmul(v_all[:], lhsT=v[b][:].to_broadcast([P, P]), rhs=identity[:], start=True, stop=True)
            plan = small.tile([P, P], F32, name="plan%d" % b)
            nc.vector.tensor_tensor(out=plan[:], in0=kern_u[b][:], in1=v_all[:], op=ALU.mult)
            nc.sync.dma_start(out=out_0[b], in_=plan[:])
        ot_sum = psum.tile([P, 1], F32, tag="bank")
        for b in range(BATCH):
            nc.tensor.matmul(
                ot_sum[:], lhsT=w[b][:].to_broadcast([P, P]), rhs=v[b][:], start=(b == 0), stop=(b == BATCH - 1)
            )
        ot_cost = small.tile([P, 1], F32)
        nc.scalar.activation(out=ot_cost[:], in_=ot_sum[:], func=ACT.Copy, scale=1.0 / BATCH)
        ot_dst = out_1
        for missing in range(2 - out_1.ndim):
            ot_dst = ot_dst.unsqueeze(0)
        nc.sync.dma_start(out=ot_dst, in_=ot_cost[0:1, 0:1])
